import numpy as np
import ml_dtypes


def mxq(x, axis, fmt="e4m3"):
    dtype, down = {"e4m3": (ml_dtypes.float8_e4m3fn, 7), "e5m2": (ml_dtypes.float8_e5m2, 14)}[fmt]
    v = np.moveaxis(np.asarray(x, np.float32).astype(ml_dtypes.bfloat16).astype(np.float64), axis, -1)
    blocks = v.reshape(v.shape[:-1] + (-1, 32))
    amax = np.abs(blocks).max(-1, keepdims=True)
    byte = np.maximum(np.where(amax > 0, np.frexp(amax)[1] - 1 + 127, 0) - down, 1)
    scale = np.exp2(byte - 127.0)
    codes = (blocks / scale).astype(np.float32).astype(dtype).astype(np.float64)
    return np.moveaxis((codes * scale).reshape(v.shape), -1, axis)


WIDE = False


def mx_kscale(k):
    if not WIDE:
        return np.ones(k)
    levels = np.array([10, -10, 5, -5, 0])
    a = np.random.permutation(np.resize(levels, k // 512 * 4)).reshape(k // 512, 4)
    idx = np.arange(k)
    return np.exp2(a[idx // 512, idx % 128 // 32])


BF16 = ml_dtypes.bfloat16


def bf(x):
    return np.asarray(x, np.float32).astype(BF16)


def f64(x):
    return np.asarray(x).astype(np.float64)


B, N, D, O, M = 4, 512, 768, 768, 4


def setup_inputs():
    s = mx_kscale(N)
    t = s / s.min()
    eye = np.eye(N)
    adj = np.exp(2.0 * np.random.standard_normal((N, N)) - 2.0) * (3.0 / N)
    adj = (t * t)[:, None] * (adj + eye) - eye
    return {"inputs": bf(np.random.standard_normal((B, N, D)) / s[None, :, None]), "adj": bf(adj)}


def reference(inputs, adj):
    x0 = f64(inputs)
    m = f64(adj) + np.eye(N)
    d = m.sum(axis=1) ** -0.5
    support = (m * d[None, :]).T * d[None, :]
    sq = mxq(support, 1, "e4m3")
    x1 = sq @ mxq(x0, 1, "e4m3")
    x2 = 2.0 * (sq @ mxq(x1, 1, "e4m3")) - x0
    return x1, x2

@@ -1,0 +1,294 @@
+from contextlib import ExitStack
+
+import concourse.mybir as mybir
+from concourse.masks import make_identity
+
+FP8X4 = mybir.dt.float8_e4m3fn_x4
+BF16 = mybir.dt.bfloat16
+F32 = mybir.dt.float32
+U32 = mybir.dt.uint32
+U8 = mybir.dt.uint8
+ALU = mybir.AluOpType
+ACT = mybir.ActivationFunctionType
+AX = mybir.AxisListType
+
+P = 128
+PACK = 4
+BATCH = 4
+NODES = 512
+FEAT = 768
+BLK = 256
+PER_BATCH = FEAT // BLK
+N_BLOCKS = BATCH * PER_BATCH
+HALF = 128
+DIAG_PITCH = NODES + P
+
+FLOPS = 2 * 2 * BATCH * NODES * NODES * FEAT
+
+PIN = False
+LEAD = 4
+SCALAR_IL = (8, 9)
+
+
+def tile_dgcn_pa_kernel(tc, inputs, adj, out_0, out_1):
+    nc = tc.nc
+    with ExitStack() as ctx:
+        keep = ctx.enter_context(tc.tile_pool(name="keep", bufs=1))
+        stage = ctx.enter_context(tc.tile_pool(name="stage", bufs=4))
+        codes = ctx.enter_context(tc.tile_pool(name="codes", bufs=6))
+        outs = ctx.enter_context(tc.tile_pool(name="outs", bufs=BATCH))
+        ps1 = ctx.enter_context(tc.psum_pool(name="ps1", bufs=4))
+        ps2 = ctx.enter_context(tc.psum_pool(name="ps2", bufs=4))
+        if PIN:
+            ctx.enter_context(tc.manual_schedule())
+
+        a_raw = keep.tile([P, PACK, NODES], BF16)
+        nc.sync.dma_start(out=a_raw[:], in_=adj.rearrange("(p t) i -> p t i", t=PACK))
+        xr = []
+        for b in range(BATCH):
+            x_b = keep.tile([P, PACK, FEAT], BF16, name="xr%d" % b)
+            nc.sync.dma_start(out=x_b[:], in_=inputs[b].rearrange("(p t) f -> p t f", t=PACK))
+            xr.append(x_b)
+
+        ident = keep.tile([P, P], F32)
+        make_identity(nc, ident[:])
+        warm = keep.tile([P, 8], F32)
+        nc.vector.memset(warm[:], 1.0)
+        warm2 = keep.tile([P, 8], F32)
+        nc.scalar.activation(out=warm2[:], in_=warm[:], func=ACT.Sqrt)
+
+        mf = keep.tile([P, PACK * DIAG_PITCH], F32)
+        mfp = mf[:, 0 : PACK * NODES].rearrange("p (t c) -> p t c", t=PACK)
+        rs = keep.tile([P, 16], F32)
+        sq = keep.tile([P, PACK], F32)
+        dcol = keep.tile([P, PACK], F32)
+        t1 = keep.tile([P, PACK, NODES], F32)
+        gs = keep.tile([P, NODES, PACK], BF16, align_bytes=64)
+        sc = keep.tile([P, NODES], U32, align_bytes=64)
+        ss = keep.tile([P, NODES], U8, align_bytes=64)
+
+        nc.vector.tensor_reduce(out=rs[:, 0:2], in_=a_raw[:, 0:2, :], axis=AX.X, op=ALU.add)
+        for t in (2, 3):
+            nc.scalar.activation(
+                out=mfp[:, t, :].rearrange("p (u q) -> p u q", u=PACK),
+                in_=a_raw[:, t, :].rearrange("p (q u) -> p u q", u=PACK),
+                func=ACT.Copy,
+                accum_out=rs[:, 6 + t : 7 + t],
+            )
+        nc.vector.tensor_copy(
+            out=mfp[:, 0:2, :].rearrange("p t (u q) -> p t u q", u=PACK),
+            in_=a_raw[:, 0:2, :].rearrange("p t (q u) -> p t u q", u=PACK),
+        )
+        nc.scalar.activation(
+            out=sq[:].rearrange("p (a b) -> p a b", a=2),
+            in_=rs[:].rearrange("p (a b) -> p a b", a=2)[:, :, 0:2],
+            func=ACT.Sqrt,
+            bias=1.0,
+            scale=1.0,
+        )
+        diag = mf[:].rearrange("p (t w) -> p t w", w=DIAG_PITCH)[:, :, 0:P]
+        nc.vector.tensor_tensor(
+            out=diag, in0=diag, in1=ident[:].unsqueeze(1).to_broadcast([P, PACK, P]), op=ALU.add
+        )
+        nc.vector.reciprocal(out=dcol[:], in_=sq[:])
+        drow = ps2.tile([P, NODES], F32, tag="p2")
+        for u in range(PACK):
+            nc.tensor.transpose(
+                out=drow[:, u * P : (u + 1) * P],
+                in_=dcol[:, u : u + 1].to_broadcast([P, P]),
+                identity=ident[:],
+            )
+        for t in range(PACK):
+            nc.vector.tensor_scalar(
+                out=t1[:, t, :], in0=mfp[:, t, :], scalar1=dcol[:, t : t + 1], scalar2=None, op0=ALU.mult
+            )
+
+        g0 = {}
+        c0 = {}
+        s0 = {}
+        g1 = {}
+        c1 = {}
+        s1 = {}
+        p1 = {}
+        p2 = {}
+        x1f = {}
+        x2f = {}
+
+        def where(n):
+            b, j = divmod(n, PER_BATCH)
+            return b, j * BLK
+
+        def regroup(n):
+            b, f0 = where(n)
+            g = stage.tile([P, BLK, PACK], BF16, name="g0_%d" % n, tag="g0", align_bytes=64)
+            nc.scalar.copy(
+                out=g[:].rearrange("p (c i) t -> p c t i", i=4),
+                in_=xr[b][:, :, f0 : f0 + BLK].rearrange("p t (c i) -> p c t i", i=4),
+            )
+            g0[n] = g
+
+        def quant(n, grouped, cdict, sdict, kind):
+            c = codes.tile([P, BLK], U32, name="c%s_%d" % (kind, n), tag="c" + kind, align_bytes=64)
+            s = codes.tile([P, BLK], U8, name="s%s_%d" % (kind, n), tag="s" + kind, align_bytes=64)
+            nc.vector.quantize_mx(
+                out=c[:].bitcast(FP8X4), scales=s[:], in_=grouped[n][:].rearrange("p f t -> p (f t)")
+            )
+            cdict[n] = c
+            sdict[n] = s
+
+        def support_piece(u):
+            cols = slice(u * P, (u + 1) * P)
+            nc.vector.tensor_tensor(
+                out=gs[:, cols, :],
+                in0=t1[:, :, cols].rearrange("p t q -> p q t"),
+                in1=drow[:, cols].unsqueeze(2).to_broadcast([P, P, PACK]),
+                op=ALU.mult,
+            )
+
+        def support_quant(u):
+            cols = slice(u * P, (u + 1) * P)
+            nc.vector.quantize_mx(
+                out=sc[:, cols].bitcast(FP8X4),
+                scales=ss[:, cols],
+                in_=gs[:, cols, :].rearrange("p q t -> p (q t)"),
+            )
+
+        def mm1(n):
+            banks = []
+            for h in range(2):
+                bank = ps1.tile([P, PACK, HALF], F32, name="p1_%d_%d" % (n, h), tag="p1")
+                cols = slice(h * HALF, (h + 1) * HALF)
+                for u in range(PACK):
+                    rows = slice(u * P, (u + 1) * P)
+                    nc.tensor.matmul_mx(
+                        out=bank[:, u, :],
+                        lhsT=sc[:, rows].bitcast(FP8X4),
+                        lhsT_scale=ss[:, rows],
+                        rhs=c0[n][:, cols].bitcast(FP8X4),
+                        rhs_scale=s0[n][:, cols],
+                        start=True,
+                        stop=True,
+                    )
+                banks.append(bank)
+            p1[n] = banks
+
+        def exit1(n):
+            b, f0 = where(n)
+            if f0 == 0:
+                x1f[b] = outs.tile([P, PACK, FEAT], F32, name="x1f%d" % b, tag="x1f")
+            for h in range(2):
+                nc.scalar.copy(
+                    out=x1f[b][:, :, f0 + h * HALF : f0 + (h + 1) * HALF], in_=p1[n][h][:]
+                )
+
+        def interleave(n):
+            b, f0 = where(n)
+            g = stage.tile([P, BLK, PACK], BF16, name="g1_%d" % n, tag="g1", align_bytes=64)
+            if n in SCALAR_IL:
+                for h in range(2):
+                    nc.scalar.copy(
+                        out=g[:, h * HALF : (h + 1) * HALF, :],
+                        in_=p1[n][h][:].rearrange("p t f -> p f t"),
+                    )
+            else:
+                nc.vector.tensor_copy(
+                    out=g[:].rearrange("p (c i) t -> p c t i", i=4),
+                    in_=x1f[b][:, :, f0 : f0 + BLK].rearrange("p t (c i) -> p c t i", i=4),
+                )
+            g1[n] = g
+
+        def mm2(n):
+            banks = []
+            for v in range(2):
+                bank = ps2.tile([P, 2, BLK], F32, name="p2_%d_%d" % (n, v), tag="p2")
+                for w in range(2):
+                    u = 2 * v + w
+                    rows = slice(u * P, (u + 1) * P)
+                    nc.tensor.matmul_mx(
+                        out=bank[:, w, :],
+                        lhsT=sc[:, rows].bitcast(FP8X4),
+                        lhsT_scale=ss[:, rows],
+                        rhs=c1[n][:].bitcast(FP8X4),
+                        rhs_scale=s1[n][:],
+                        start=True,
+                        stop=True,
+                    )
+                banks.append(bank)
+            p2[n] = banks
+
+        def exit2(n, v):
+            b, f0 = where(n)
+            if f0 == 0 and v == 0:
+                x2f[b] = outs.tile([P, PACK, FEAT], F32, name="x2f%d" % b, tag="x2f")
+            nc.vector.scalar_tensor_tensor(
+                out=x2f[b][:, 2 * v : 2 * v + 2, f0 : f0 + BLK],
+                in0=p2[n][v][:],
+                scalar=2.0,
+                in1=xr[b][:, 2 * v : 2 * v + 2, f0 : f0 + BLK],
+                op0=ALU.mult,
+                op1=ALU.subtract,
+            )
+
+        def store(dram, sb, b, lo, hi):
+            nc.sync.dma_start(
+                out=dram[b].rearrange("(p t) f -> p t f", t=PACK)[:, :, lo:hi], in_=sb[b][:, :, lo:hi]
+            )
+
+        def store1(n):
+            b, f0 = where(n)
+            if b == 0:
+                store(out_0, x1f, b, f0, f0 + BLK)
+            elif f0 + BLK == FEAT:
+                store(out_0, x1f, b, 0, FEAT)
+
+        def store2(n):
+            b, f0 = where(n)
+            if b == BATCH - 1:
+                if f0 == BLK:
+                    store(out_1, x2f, b, 0, 2 * BLK)
+                elif f0 == 2 * BLK:
+                    store(out_1, x2f, b, 2 * BLK, FEAT)
+            elif f0 + BLK == FEAT:
+                store(out_1, x2f, b, 0, FEAT)
+
+        for n in range(LEAD):
+            regroup(n)
+        support_piece(0)
+        quant(0, g0, c0, s0, "0")
+        support_piece(1)
+        support_quant(0)
+        support_piece(2)
+        support_quant(1)
+        support_piece(3)
+        support_quant(2)
+        quant(1, g0, c0, s0, "0")
+        support_quant(3)
+        quant(2, g0, c0, s0, "0")
+        quant(3, g0, c0, s0, "0")
+        mm1(0)
+        mm1(1)
+
+        for n in range(N_BLOCKS):
+            exit1(n)
+            store1(n)
+            if n in SCALAR_IL:
+                interleave(n)
+            if n + LEAD < N_BLOCKS:
+                regroup(n + LEAD)
+            if n + 2 < N_BLOCKS:
+                mm1(n + 2)
+            if n not in SCALAR_IL:
+                interleave(n)
+            if n >= 2:
+                exit2(n - 2, 0)
+            quant(n, g1, c1, s1, "1")
+            if n >= 2:
+                exit2(n - 2, 1)
+                store2(n - 2)
+            if n + LEAD < N_BLOCKS:
+                quant(n + LEAD, g0, c0, s0, "0")
+            mm2(n)
+        for n in (N_BLOCKS - 2, N_BLOCKS - 1):
+            exit2(n, 0)
+            exit2(n, 1)
+            store2(n)

@@ -20,22 +20,56 @@ FEAT = 768
 BLK = 256
 PER_BATCH = FEAT // BLK
 N_BLOCKS = BATCH * PER_BATCH
-HALF = 128
 DIAG_PITCH = NODES + P
 
 FLOPS = 2 * 2 * BATCH * NODES * NODES * FEAT
 
-PIN = False
-LEAD = 4
-SCALAR_IL = (8, 9)
+PIN = True
+SUM_COL = {1: 0, 3: 1, 0: 2, 2: 3}
+RAW_COL = {1: 0, 3: 1, 0: 8, 2: 9}
+
+ORDER = (
+    ("ld_a", 0), ("ld_a", 1), ("ld_a", 2), ("ld_a", 3), ("ld_x", 0), ("ld_x", 1),
+    ("ld_x", 2), ("ld_x", 3), ("act", 0), ("red", 1), ("act", 2), ("red", 3),
+    ("cast", 0), ("sqrt", 0), ("recip", 0), ("diag", 0), ("tr", 0), ("tr", 1),
+    ("rgS", 0), ("tr", 2), ("t1", 0), ("tr", 3), ("t1", 1), ("t1", 2),
+    ("rgS", 1), ("t1", 3), ("gp", 0), ("rgS", 2), ("q0", 0), ("gp", 1),
+    ("qs", 0), ("rgS", 3), ("gp", 2), ("qs", 1), ("gp", 3), ("rgS", 4),
+    ("qs", 2), ("qs", 3), ("q0", 1), ("q0", 2), ("mm1", 0), ("q0", 3),
+    ("mm1", 1), ("e1", 0), ("q0", 4), ("mm1", 2), ("rgV", 5), ("mm1", 3),
+    ("e1", 1), ("mm1", 4), ("rgV", 6), ("e1", 2), ("mm1", 5), ("q0", 5),
+    ("e1", 3), ("mm1", 6), ("st1", 0), ("rgV", 7), ("e1", 4), ("mm1", 7),
+    ("q0", 6), ("rgV", 8), ("e1", 5), ("mm1", 8), ("q0", 7), ("e1", 6),
+    ("mm1", 9), ("st1", 1), ("ilV", 0), ("e1", 7), ("mm1", 10), ("q0", 8),
+    ("e1", 8), ("ilV", 1), ("mm1", 11), ("e1", 9), ("ilV", 2), ("mm1", 12),
+    ("st1", 2), ("e1", 10), ("mm1", 13), ("q1", 0), ("q1", 1), ("e1", 11),
+    ("mm1", 14), ("q1", 2), ("mm2", 0), ("rgV", 9), ("e1", 12), ("mm2", 1),
+    ("st1", 3), ("mm2", 2), ("rgV", 10), ("e1", 13), ("mm2", 3), ("mm1", 15),
+    ("q0", 9), ("e1", 14), ("mm1", 16), ("rgV", 11), ("mm1", 17), ("e1", 15),
+    ("mm1", 18), ("st1", 4), ("q0", 10), ("e1", 16), ("q0", 11), ("e2", 0),
+    ("mm1", 19), ("e1", 17), ("mm1", 20), ("e2", 1), ("mm2", 4), ("e1", 18),
+    ("st1", 5), ("mm1", 21), ("e2", 2), ("e1", 19), ("mm2", 5), ("mm1", 22),
+    ("e2", 3), ("e1", 20), ("st2", 0), ("mm1", 23), ("e2", 4), ("e1", 21),
+    ("st1", 6), ("e2", 5), ("e1", 22), ("e1", 23), ("ilV", 3), ("st2", 1),
+    ("ilS", 5), ("ilV", 4), ("st1", 7), ("q1", 3), ("q1", 4), ("ilS", 6),
+    ("q1", 5), ("mm2", 6), ("mm2", 7), ("e2", 6), ("mm2", 8), ("mm2", 9),
+    ("ilS", 7), ("e2", 7), ("mm2", 10), ("e2", 8), ("mm2", 11), ("ilS", 8),
+    ("e2", 9), ("st2", 2), ("e2", 10), ("ilS", 9), ("e2", 11), ("q1", 6),
+    ("st2", 3), ("q1", 7), ("ilS", 10), ("q1", 8), ("mm2", 12), ("mm2", 13),
+    ("e2", 12), ("mm2", 14), ("mm2", 15), ("ilS", 11), ("e2", 13), ("mm2", 16),
+    ("e2", 14), ("mm2", 17), ("e2", 15), ("st2", 4), ("e2", 16), ("e2", 17),
+    ("q1", 9), ("st2", 5), ("q1", 10), ("q1", 11), ("mm2", 18), ("mm2", 19),
+    ("e2", 18), ("mm2", 20), ("mm2", 21), ("e2", 19), ("mm2", 22), ("e2", 20),
+    ("mm2", 23), ("e2", 21), ("st2", 6), ("e2", 22), ("e2", 23), ("st2", 7),
+)
 
 
 def tile_dgcn_pa_kernel(tc, inputs, adj, out_0, out_1):
     nc = tc.nc
     with ExitStack() as ctx:
         keep = ctx.enter_context(tc.tile_pool(name="keep", bufs=1))
-        stage = ctx.enter_context(tc.tile_pool(name="stage", bufs=4))
-        codes = ctx.enter_context(tc.tile_pool(name="codes", bufs=6))
+        stage = ctx.enter_context(tc.tile_pool(name="stage", bufs=6))
+        codes = ctx.enter_context(tc.tile_pool(name="codes", bufs=N_BLOCKS))
         outs = ctx.enter_context(tc.tile_pool(name="outs", bufs=BATCH))
         ps1 = ctx.enter_context(tc.psum_pool(name="ps1", bufs=4))
         ps2 = ctx.enter_context(tc.psum_pool(name="ps2", bufs=4))
@@ -43,13 +77,11 @@ def tile_dgcn_pa_kernel(tc, inputs, adj, out_0, out_1):
             ctx.enter_context(tc.manual_schedule())
 
         a_raw = keep.tile([P, PACK, NODES], BF16)
-        nc.sync.dma_start(out=a_raw[:], in_=adj.rearrange("(p t) i -> p t i", t=PACK))
+        adj_v = adj.rearrange("(p t) i -> p t i", t=PACK)
         xr = []
         for b in range(BATCH):
             x_b = keep.tile([P, PACK, FEAT], BF16, name="xr%d" % b)
-            nc.sync.dma_start(out=x_b[:], in_=inputs[b].rearrange("(p t) f -> p t f", t=PACK))
             xr.append(x_b)
-
         ident = keep.tile([P, P], F32)
         make_identity(nc, ident[:])
         warm = keep.tile([P, 8], F32)
@@ -66,42 +98,7 @@ def tile_dgcn_pa_kernel(tc, inputs, adj, out_0, out_1):
         gs = keep.tile([P, NODES, PACK], BF16, align_bytes=64)
         sc = keep.tile([P, NODES], U32, align_bytes=64)
         ss = keep.tile([P, NODES], U8, align_bytes=64)
-
-        nc.vector.tensor_reduce(out=rs[:, 0:2], in_=a_raw[:, 0:2, :], axis=AX.X, op=ALU.add)
-        for t in (2, 3):
-            nc.scalar.activation(
-                out=mfp[:, t, :].rearrange("p (u q) -> p u q", u=PACK),
-                in_=a_raw[:, t, :].rearrange("p (q u) -> p u q", u=PACK),
-                func=ACT.Copy,
-                accum_out=rs[:, 6 + t : 7 + t],
-            )
-        nc.vector.tensor_copy(
-            out=mfp[:, 0:2, :].rearrange("p t (u q) -> p t u q", u=PACK),
-            in_=a_raw[:, 0:2, :].rearrange("p t (q u) -> p t u q", u=PACK),
-        )
-        nc.scalar.activation(
-            out=sq[:].rearrange("p (a b) -> p a b", a=2),
-            in_=rs[:].rearrange("p (a b) -> p a b", a=2)[:, :, 0:2],
-            func=ACT.Sqrt,
-            bias=1.0,
-            scale=1.0,
-        )
-        diag = mf[:].rearrange("p (t w) -> p t w", w=DIAG_PITCH)[:, :, 0:P]
-        nc.vector.tensor_tensor(
-            out=diag, in0=diag, in1=ident[:].unsqueeze(1).to_broadcast([P, PACK, P]), op=ALU.add
-        )
-        nc.vector.reciprocal(out=dcol[:], in_=sq[:])
         drow = ps2.tile([P, NODES], F32, tag="p2")
-        for u in range(PACK):
-            nc.tensor.transpose(
-                out=drow[:, u * P : (u + 1) * P],
-                in_=dcol[:, u : u + 1].to_broadcast([P, P]),
-                identity=ident[:],
-            )
-        for t in range(PACK):
-            nc.vector.tensor_scalar(
-                out=t1[:, t, :], in0=mfp[:, t, :], scalar1=dcol[:, t : t + 1], scalar2=None, op0=ALU.mult
-            )
 
         g0 = {}
         c0 = {}
@@ -118,14 +115,102 @@ def tile_dgcn_pa_kernel(tc, inputs, adj, out_0, out_1):
             b, j = divmod(n, PER_BATCH)
             return b, j * BLK
 
-        def regroup(n):
+        def bank_of(k):
+            b, r = divmod(k, 2 * PER_BATCH)
+            v, j = divmod(r, PER_BATCH)
+            return b, v, j
+
+        def ld_a(t):
+            nc.sync.dma_start(out=a_raw[:, t, :], in_=adj_v[:, t, :])
+
+        def ld_x(b):
+            nc.sync.dma_start(out=xr[b][:], in_=inputs[b].rearrange("(p t) f -> p t f", t=PACK))
+
+        def act(t):
+            nc.scalar.activation(
+                out=mfp[:, t, :].rearrange("p (u q) -> p u q", u=PACK),
+                in_=a_raw[:, t, :].rearrange("p (q u) -> p u q", u=PACK),
+                func=ACT.Copy,
+                accum_out=rs[:, RAW_COL[t] : RAW_COL[t] + 1],
+            )
+
+        def red(t):
+            nc.vector.tensor_reduce(
+                out=rs[:, RAW_COL[t] : RAW_COL[t] + 1], in_=a_raw[:, t, :], axis=AX.X, op=ALU.add
+            )
+
+        def cast(z):
+            nc.vector.tensor_copy(
+                out=mfp.rearrange("p (a e) (u q) -> p a e u q", e=2, u=PACK)[:, :, 1, :, :],
+                in_=a_raw[:].rearrange("p (a e) (q u) -> p a e u q", e=2, u=PACK)[:, :, 1, :, :],
+            )
+
+        def sqrt(z):
+            nc.scalar.activation(
+                out=sq[:].rearrange("p (a e) -> p a e", a=2),
+                in_=rs[:].rearrange("p (a e) -> p a e", a=2)[:, :, 0:2],
+                func=ACT.Sqrt,
+                bias=1.0,
+                scale=1.0,
+            )
+
+        def diag(z):
+            view = mf[:].rearrange("p (t w) -> p t w", w=DIAG_PITCH)[:, :, 0:P]
+            nc.vector.tensor_tensor(
+                out=view, in0=view, in1=ident[:].unsqueeze(1).to_broadcast([P, PACK, P]), op=ALU.add
+            )
+
+        def recip(z):
+            nc.vector.reciprocal(out=dcol[:], in_=sq[:])
+
+        def tr(u):
+            c = SUM_COL[u]
+            nc.tensor.transpose(
+                out=drow[:, u * P : (u + 1) * P],
+                in_=dcol[:, c : c + 1].to_broadcast([P, P]),
+                identity=ident[:],
+            )
+
+        def t1_op(t):
+            c = SUM_COL[t]
+            nc.vector.tensor_scalar(
+                out=t1[:, t, :], in0=mfp[:, t, :], scalar1=dcol[:, c : c + 1], scalar2=None, op0=ALU.mult
+            )
+
+        def gp(u):
+            cols = slice(u * P, (u + 1) * P)
+            nc.vector.tensor_tensor(
+                out=gs[:, cols, :],
+                in0=t1[:, :, cols].rearrange("p t q -> p q t"),
+                in1=drow[:, cols].unsqueeze(2).to_broadcast([P, P, PACK]),
+                op=ALU.mult,
+            )
+
+        def qs(u):
+            cols = slice(u * P, (u + 1) * P)
+            nc.vector.quantize_mx(
+                out=sc[:, cols].bitcast(FP8X4),
+                scales=ss[:, cols],
+                in_=gs[:, cols, :].rearrange("p q t -> p (q t)"),
+            )
+
+        def regroup(n, eng_copy):
             b, f0 = where(n)
             g = stage.tile([P, BLK, PACK], BF16, name="g0_%d" % n, tag="g0", align_bytes=64)
-            nc.scalar.copy(
+            eng_copy(
                 out=g[:].rearrange("p (c i) t -> p c t i", i=4),
                 in_=xr[b][:, :, f0 : f0 + BLK].rearrange("p t (c i) -> p c t i", i=4),
             )
             g0[n] = g
+
+        def interleave(n, eng_copy):
+            b, f0 = where(n)
+            g = stage.tile([P, BLK, PACK], BF16, name="g1_%d" % n, tag="g1", align_bytes=64)
+            eng_copy(
+                out=g[:].rearrange("p (c i) t -> p c t i", i=4),
+                in_=x1f[b][:, :, f0 : f0 + BLK].rearrange("p t (c i) -> p c t i", i=4),
+            )
+            g1[n] = g
 
         def quant(n, grouped, cdict, sdict, kind):
             c = codes.tile([P, BLK], U32, name="c%s_%d" % (kind, n), tag="c" + kind, align_bytes=64)
@@ -136,159 +221,77 @@ def tile_dgcn_pa_kernel(tc, inputs, adj, out_0, out_1):
             cdict[n] = c
             sdict[n] = s
 
-        def support_piece(u):
-            cols = slice(u * P, (u + 1) * P)
-            nc.vector.tensor_tensor(
-                out=gs[:, cols, :],
-                in0=t1[:, :, cols].rearrange("p t q -> p q t"),
-                in1=drow[:, cols].unsqueeze(2).to_broadcast([P, P, PACK]),
-                op=ALU.mult,
-            )
+        def mm(k, pool, tag, cdict, sdict, banks):
+            b, v, j = bank_of(k)
+            n = b * PER_BATCH + j
+            bank = pool.tile([P, 2, BLK], F32, name="%s_%d" % (tag, k), tag=tag)
+            for w in range(2):
+                u = 2 * v + w
+                rows = slice(u * P, (u + 1) * P)
+                nc.tensor.matmul_mx(
+                    out=bank[:, w, :],
+                    lhsT=sc[:, rows].bitcast(FP8X4),
+                    lhsT_scale=ss[:, rows],
+                    rhs=cdict[n][:].bitcast(FP8X4),
+                    rhs_scale=sdict[n][:],
+                    start=True,
+                    stop=True,
+                )
+            banks[k] = bank
 
-        def support_quant(u):
-            cols = slice(u * P, (u + 1) * P)
-            nc.vector.quantize_mx(
-                out=sc[:, cols].bitcast(FP8X4),
-                scales=ss[:, cols],
-                in_=gs[:, cols, :].rearrange("p q t -> p (q t)"),
-            )
-
-        def mm1(n):
-            banks = []
-            for h in range(2):
-                bank = ps1.tile([P, PACK, HALF], F32, name="p1_%d_%d" % (n, h), tag="p1")
-                cols = slice(h * HALF, (h + 1) * HALF)
-                for u in range(PACK):
-                    rows = slice(u * P, (u + 1) * P)
-                    nc.tensor.matmul_mx(
-                        out=bank[:, u, :],
-                        lhsT=sc[:, rows].bitcast(FP8X4),
-                        lhsT_scale=ss[:, rows],
-                        rhs=c0[n][:, cols].bitcast(FP8X4),
-                        rhs_scale=s0[n][:, cols],
-                        start=True,
-                        stop=True,
-                    )
-                banks.append(bank)
-            p1[n] = banks
-
-        def exit1(n):
-            b, f0 = where(n)
-            if f0 == 0:
+        def e1(k):
+            b, v, j = bank_of(k)
+            if v == 0 and j == 0:
                 x1f[b] = outs.tile([P, PACK, FEAT], F32, name="x1f%d" % b, tag="x1f")
-            for h in range(2):
-                nc.scalar.copy(
-                    out=x1f[b][:, :, f0 + h * HALF : f0 + (h + 1) * HALF], in_=p1[n][h][:]
-                )
+            nc.scalar.copy(
+                out=x1f[b][:, 2 * v : 2 * v + 2, j * BLK : (j + 1) * BLK], in_=p1[k][:]
+            )
 
-        def interleave(n):
-            b, f0 = where(n)
-            g = stage.tile([P, BLK, PACK], BF16, name="g1_%d" % n, tag="g1", align_bytes=64)
-            if n in SCALAR_IL:
-                for h in range(2):
-                    nc.scalar.copy(
-                        out=g[:, h * HALF : (h + 1) * HALF, :],
-                        in_=p1[n][h][:].rearrange("p t f -> p f t"),
-                    )
-            else:
-                nc.vector.tensor_copy(
-                    out=g[:].rearrange("p (c i) t -> p c t i", i=4),
-                    in_=x1f[b][:, :, f0 : f0 + BLK].rearrange("p t (c i) -> p c t i", i=4),
-                )
-            g1[n] = g
-
-        def mm2(n):
-            banks = []
-            for v in range(2):
-                bank = ps2.tile([P, 2, BLK], F32, name="p2_%d_%d" % (n, v), tag="p2")
-                for w in range(2):
-                    u = 2 * v + w
-                    rows = slice(u * P, (u + 1) * P)
-                    nc.tensor.matmul_mx(
-                        out=bank[:, w, :],
-                        lhsT=sc[:, rows].bitcast(FP8X4),
-                        lhsT_scale=ss[:, rows],
-                        rhs=c1[n][:].bitcast(FP8X4),
-                        rhs_scale=s1[n][:],
-                        start=True,
-                        stop=True,
-                    )
-                banks.append(bank)
-            p2[n] = banks
-
-        def exit2(n, v):
-            b, f0 = where(n)
-            if f0 == 0 and v == 0:
+        def e2(k):
+            b, v, j = bank_of(k)
+            if v == 0 and j == 0:
                 x2f[b] = outs.tile([P, PACK, FEAT], F32, name="x2f%d" % b, tag="x2f")
             nc.vector.scalar_tensor_tensor(
-                out=x2f[b][:, 2 * v : 2 * v + 2, f0 : f0 + BLK],
-                in0=p2[n][v][:],
+                out=x2f[b][:, 2 * v : 2 * v + 2, j * BLK : (j + 1) * BLK],
+                in0=p2[k][:],
                 scalar=2.0,
-                in1=xr[b][:, 2 * v : 2 * v + 2, f0 : f0 + BLK],
+                in1=xr[b][:, 2 * v : 2 * v + 2, j * BLK : (j + 1) * BLK],
                 op0=ALU.mult,
                 op1=ALU.subtract,
             )
 
-        def store(dram, sb, b, lo, hi):
+        def store(dram, sb, h):
+            b, v = divmod(h, 2)
             nc.sync.dma_start(
-                out=dram[b].rearrange("(p t) f -> p t f", t=PACK)[:, :, lo:hi], in_=sb[b][:, :, lo:hi]
+                out=dram[b].rearrange("(p t) f -> p t f", t=PACK)[:, 2 * v : 2 * v + 2, :],
+                in_=sb[b][:, 2 * v : 2 * v + 2, :],
             )
 
-        def store1(n):
-            b, f0 = where(n)
-            if b == 0:
-                store(out_0, x1f, b, f0, f0 + BLK)
-            elif f0 + BLK == FEAT:
-                store(out_0, x1f, b, 0, FEAT)
-
-        def store2(n):
-            b, f0 = where(n)
-            if b == BATCH - 1:
-                if f0 == BLK:
-                    store(out_1, x2f, b, 0, 2 * BLK)
-                elif f0 == 2 * BLK:
-                    store(out_1, x2f, b, 2 * BLK, FEAT)
-            elif f0 + BLK == FEAT:
-                store(out_1, x2f, b, 0, FEAT)
-
-        for n in range(LEAD):
-            regroup(n)
-        support_piece(0)
-        quant(0, g0, c0, s0, "0")
-        support_piece(1)
-        support_quant(0)
-        support_piece(2)
-        support_quant(1)
-        support_piece(3)
-        support_quant(2)
-        quant(1, g0, c0, s0, "0")
-        support_quant(3)
-        quant(2, g0, c0, s0, "0")
-        quant(3, g0, c0, s0, "0")
-        mm1(0)
-        mm1(1)
-
-        for n in range(N_BLOCKS):
-            exit1(n)
-            store1(n)
-            if n in SCALAR_IL:
-                interleave(n)
-            if n + LEAD < N_BLOCKS:
-                regroup(n + LEAD)
-            if n + 2 < N_BLOCKS:
-                mm1(n + 2)
-            if n not in SCALAR_IL:
-                interleave(n)
-            if n >= 2:
-                exit2(n - 2, 0)
-            quant(n, g1, c1, s1, "1")
-            if n >= 2:
-                exit2(n - 2, 1)
-                store2(n - 2)
-            if n + LEAD < N_BLOCKS:
-                quant(n + LEAD, g0, c0, s0, "0")
-            mm2(n)
-        for n in (N_BLOCKS - 2, N_BLOCKS - 1):
-            exit2(n, 0)
-            exit2(n, 1)
-            store2(n)
+        ops = {
+            "ld_a": ld_a,
+            "ld_x": ld_x,
+            "act": act,
+            "red": red,
+            "cast": cast,
+            "sqrt": sqrt,
+            "diag": diag,
+            "recip": recip,
+            "tr": tr,
+            "t1": t1_op,
+            "gp": gp,
+            "qs": qs,
+            "rgS": lambda n: regroup(n, nc.scalar.copy),
+            "rgV": lambda n: regroup(n, nc.vector.tensor_copy),
+            "ilS": lambda n: interleave(n, nc.scalar.copy),
+            "ilV": lambda n: interleave(n, nc.vector.tensor_copy),
+            "q0": lambda n: quant(n, g0, c0, s0, "0"),
+            "q1": lambda n: quant(n, g1, c1, s1, "1"),
+            "mm1": lambda k: mm(k, ps1, "p1", c0, s0, p1),
+            "mm2": lambda k: mm(k, ps2, "p2", c1, s1, p2),
+            "e1": e1,
+            "e2": e2,
+            "st1": lambda h: store(out_0, x1f, h),
+            "st2": lambda h: store(out_1, x2f, h),
+        }
+        for name, arg in ORDER:
+            ops[name](arg)

@@ -13,285 +13,222 @@ ACT = mybir.ActivationFunctionType
 AX = mybir.AxisListType
 
 P = 128
-PACK = 4
+ROWS = 4
 BATCH = 4
-NODES = 512
+NODES = P * ROWS
 FEAT = 768
-BLK = 256
-PER_BATCH = FEAT // BLK
-N_BLOCKS = BATCH * PER_BATCH
-DIAG_PITCH = NODES + P
+BLOCK = 256
+BLOCKS_PER_BATCH = FEAT // BLOCK
+N_BLOCKS = BATCH * BLOCKS_PER_BATCH
+PAIRS = ROWS // 2
+BANKS_PER_BATCH = PAIRS * BLOCKS_PER_BATCH
+
+SCALAR_REGROUPS = 5
+VECTOR_INTERLEAVES = 7
 
 FLOPS = 2 * 2 * BATCH * NODES * NODES * FEAT
 
-PIN = True
-SUM_COL = {1: 0, 3: 1, 0: 2, 2: 3}
-RAW_COL = {1: 0, 3: 1, 0: 8, 2: 9}
 
-ORDER = (
-    ("ld_a", 0), ("ld_a", 1), ("ld_a", 2), ("ld_a", 3), ("ld_x", 0), ("ld_x", 1),
-    ("ld_x", 2), ("ld_x", 3), ("act", 0), ("red", 1), ("act", 2), ("red", 3),
-    ("cast", 0), ("sqrt", 0), ("recip", 0), ("diag", 0), ("tr", 0), ("tr", 1),
-    ("rgS", 0), ("tr", 2), ("t1", 0), ("tr", 3), ("t1", 1), ("t1", 2),
-    ("rgS", 1), ("t1", 3), ("gp", 0), ("rgS", 2), ("q0", 0), ("gp", 1),
-    ("qs", 0), ("rgS", 3), ("gp", 2), ("qs", 1), ("gp", 3), ("rgS", 4),
-    ("qs", 2), ("qs", 3), ("q0", 1), ("q0", 2), ("mm1", 0), ("q0", 3),
-    ("mm1", 1), ("e1", 0), ("q0", 4), ("mm1", 2), ("rgV", 5), ("mm1", 3),
-    ("e1", 1), ("mm1", 4), ("rgV", 6), ("e1", 2), ("mm1", 5), ("q0", 5),
-    ("e1", 3), ("mm1", 6), ("st1", 0), ("rgV", 7), ("e1", 4), ("mm1", 7),
-    ("q0", 6), ("rgV", 8), ("e1", 5), ("mm1", 8), ("q0", 7), ("e1", 6),
-    ("mm1", 9), ("st1", 1), ("ilV", 0), ("e1", 7), ("mm1", 10), ("q0", 8),
-    ("e1", 8), ("ilV", 1), ("mm1", 11), ("e1", 9), ("ilV", 2), ("mm1", 12),
-    ("st1", 2), ("e1", 10), ("mm1", 13), ("q1", 0), ("q1", 1), ("e1", 11),
-    ("mm1", 14), ("q1", 2), ("mm2", 0), ("rgV", 9), ("e1", 12), ("mm2", 1),
-    ("st1", 3), ("mm2", 2), ("rgV", 10), ("e1", 13), ("mm2", 3), ("mm1", 15),
-    ("q0", 9), ("e1", 14), ("mm1", 16), ("rgV", 11), ("mm1", 17), ("e1", 15),
-    ("mm1", 18), ("st1", 4), ("q0", 10), ("e1", 16), ("q0", 11), ("e2", 0),
-    ("mm1", 19), ("e1", 17), ("mm1", 20), ("e2", 1), ("mm2", 4), ("e1", 18),
-    ("st1", 5), ("mm1", 21), ("e2", 2), ("e1", 19), ("mm2", 5), ("mm1", 22),
-    ("e2", 3), ("e1", 20), ("st2", 0), ("mm1", 23), ("e2", 4), ("e1", 21),
-    ("st1", 6), ("e2", 5), ("e1", 22), ("e1", 23), ("ilV", 3), ("st2", 1),
-    ("ilS", 5), ("ilV", 4), ("st1", 7), ("q1", 3), ("q1", 4), ("ilS", 6),
-    ("q1", 5), ("mm2", 6), ("mm2", 7), ("e2", 6), ("mm2", 8), ("mm2", 9),
-    ("ilS", 7), ("e2", 7), ("mm2", 10), ("e2", 8), ("mm2", 11), ("ilS", 8),
-    ("e2", 9), ("st2", 2), ("e2", 10), ("ilS", 9), ("e2", 11), ("q1", 6),
-    ("st2", 3), ("q1", 7), ("ilS", 10), ("q1", 8), ("mm2", 12), ("mm2", 13),
-    ("e2", 12), ("mm2", 14), ("mm2", 15), ("ilS", 11), ("e2", 13), ("mm2", 16),
-    ("e2", 14), ("mm2", 17), ("e2", 15), ("st2", 4), ("e2", 16), ("e2", 17),
-    ("q1", 9), ("st2", 5), ("q1", 10), ("q1", 11), ("mm2", 18), ("mm2", 19),
-    ("e2", 18), ("mm2", 20), ("mm2", 21), ("e2", 19), ("mm2", 22), ("e2", 20),
-    ("mm2", 23), ("e2", 21), ("st2", 6), ("e2", 22), ("e2", 23), ("st2", 7),
-)
+def by_fours(rows_first, cols_first):
+    return (
+        cols_first.rearrange("p (c i) t -> p c t i", i=4),
+        rows_first.rearrange("p t (c i) -> p c t i", i=4),
+    )
 
 
 def tile_dgcn_pa_kernel(tc, inputs, adj, out_0, out_1):
     nc = tc.nc
     with ExitStack() as ctx:
         keep = ctx.enter_context(tc.tile_pool(name="keep", bufs=1))
-        stage = ctx.enter_context(tc.tile_pool(name="stage", bufs=6))
-        codes = ctx.enter_context(tc.tile_pool(name="codes", bufs=N_BLOCKS))
-        outs = ctx.enter_context(tc.tile_pool(name="outs", bufs=BATCH))
-        ps1 = ctx.enter_context(tc.psum_pool(name="ps1", bufs=4))
-        ps2 = ctx.enter_context(tc.psum_pool(name="ps2", bufs=4))
-        if PIN:
-            ctx.enter_context(tc.manual_schedule())
+        grouped = ctx.enter_context(tc.tile_pool(name="grouped", bufs=2 * BLOCKS_PER_BATCH))
+        packed = ctx.enter_context(tc.tile_pool(name="packed", bufs=N_BLOCKS))
+        results = ctx.enter_context(tc.tile_pool(name="results", bufs=BATCH))
+        psum_x1 = ctx.enter_context(tc.psum_pool(name="psum_x1", bufs=4))
+        psum_x2 = ctx.enter_context(tc.psum_pool(name="psum_x2", bufs=4))
+        ctx.enter_context(tc.manual_schedule())
 
-        a_raw = keep.tile([P, PACK, NODES], BF16)
-        adj_v = adj.rearrange("(p t) i -> p t i", t=PACK)
-        xr = []
+        adj_rows = keep.tile([P, ROWS, NODES], BF16)
+        adj_view = adj.rearrange("(p t) i -> p t i", t=ROWS)
+        for t in range(ROWS):
+            nc.sync.dma_start(out=adj_rows[:, t, :], in_=adj_view[:, t, :])
+        x0 = []
         for b in range(BATCH):
-            x_b = keep.tile([P, PACK, FEAT], BF16, name="xr%d" % b)
-            xr.append(x_b)
-        ident = keep.tile([P, P], F32)
-        make_identity(nc, ident[:])
-        warm = keep.tile([P, 8], F32)
-        nc.vector.memset(warm[:], 1.0)
-        warm2 = keep.tile([P, 8], F32)
-        nc.scalar.activation(out=warm2[:], in_=warm[:], func=ACT.Sqrt)
+            x0_b = keep.tile([P, ROWS, FEAT], BF16, name="x0_%d" % b)
+            nc.sync.dma_start(out=x0_b[:], in_=inputs[b].rearrange("(p t) f -> p t f", t=ROWS))
+            x0.append(x0_b)
 
-        mf = keep.tile([P, PACK * DIAG_PITCH], F32)
-        mfp = mf[:, 0 : PACK * NODES].rearrange("p (t c) -> p t c", t=PACK)
-        rs = keep.tile([P, 16], F32)
-        sq = keep.tile([P, PACK], F32)
-        dcol = keep.tile([P, PACK], F32)
-        t1 = keep.tile([P, PACK, NODES], F32)
-        gs = keep.tile([P, NODES, PACK], BF16, align_bytes=64)
-        sc = keep.tile([P, NODES], U32, align_bytes=64)
-        ss = keep.tile([P, NODES], U8, align_bytes=64)
-        drow = ps2.tile([P, NODES], F32, tag="p2")
+        identity = keep.tile([P, P], F32)
+        make_identity(nc, identity[:])
+        ones = keep.tile([P, 8], F32)
+        nc.vector.memset(ones[:], 1.0)
+        dummy = keep.tile([P, 8], F32)
+        nc.scalar.activation(out=dummy[:], in_=ones[:], func=ACT.Sqrt)
 
-        g0 = {}
-        c0 = {}
-        s0 = {}
-        g1 = {}
-        c1 = {}
-        s1 = {}
-        p1 = {}
-        p2 = {}
-        x1f = {}
-        x2f = {}
-
-        def where(n):
-            b, j = divmod(n, PER_BATCH)
-            return b, j * BLK
-
-        def bank_of(k):
-            b, r = divmod(k, 2 * PER_BATCH)
-            v, j = divmod(r, PER_BATCH)
-            return b, v, j
-
-        def ld_a(t):
-            nc.sync.dma_start(out=a_raw[:, t, :], in_=adj_v[:, t, :])
-
-        def ld_x(b):
-            nc.sync.dma_start(out=xr[b][:], in_=inputs[b].rearrange("(p t) f -> p t f", t=PACK))
-
-        def act(t):
-            nc.scalar.activation(
-                out=mfp[:, t, :].rearrange("p (u q) -> p u q", u=PACK),
-                in_=a_raw[:, t, :].rearrange("p (q u) -> p u q", u=PACK),
-                func=ACT.Copy,
-                accum_out=rs[:, RAW_COL[t] : RAW_COL[t] + 1],
-            )
-
-        def red(t):
-            nc.vector.tensor_reduce(
-                out=rs[:, RAW_COL[t] : RAW_COL[t] + 1], in_=a_raw[:, t, :], axis=AX.X, op=ALU.add
-            )
-
-        def cast(z):
-            nc.vector.tensor_copy(
-                out=mfp.rearrange("p (a e) (u q) -> p a e u q", e=2, u=PACK)[:, :, 1, :, :],
-                in_=a_raw[:].rearrange("p (a e) (q u) -> p a e u q", e=2, u=PACK)[:, :, 1, :, :],
-            )
-
-        def sqrt(z):
-            nc.scalar.activation(
-                out=sq[:].rearrange("p (a e) -> p a e", a=2),
-                in_=rs[:].rearrange("p (a e) -> p a e", a=2)[:, :, 0:2],
-                func=ACT.Sqrt,
-                bias=1.0,
-                scale=1.0,
-            )
-
-        def diag(z):
-            view = mf[:].rearrange("p (t w) -> p t w", w=DIAG_PITCH)[:, :, 0:P]
-            nc.vector.tensor_tensor(
-                out=view, in0=view, in1=ident[:].unsqueeze(1).to_broadcast([P, PACK, P]), op=ALU.add
-            )
-
-        def recip(z):
-            nc.vector.reciprocal(out=dcol[:], in_=sq[:])
-
-        def tr(u):
-            c = SUM_COL[u]
+        pitch = NODES + P
+        m_flat = keep.tile([P, ROWS * pitch], F32)
+        m = m_flat[:, 0 : ROWS * NODES].rearrange("p (t c) -> p t c", t=ROWS)
+        sums = keep.tile([P, 16], F32)
+        sum_at = {1: 0, 3: 1, 0: 8, 2: 9}
+        dd_at = {1: 0, 3: 1, 0: 2, 2: 3}
+        for t in range(ROWS):
+            total = sums[:, sum_at[t] : sum_at[t] + 1]
+            if t % 2 == 0:
+                nc.scalar.activation(
+                    out=m[:, t, :].rearrange("p (u q) -> p u q", u=ROWS),
+                    in_=adj_rows[:, t, :].rearrange("p (q u) -> p u q", u=ROWS),
+                    func=ACT.Copy,
+                    accum_out=total,
+                )
+            else:
+                nc.vector.tensor_reduce(out=total, in_=adj_rows[:, t, :], axis=AX.X, op=ALU.add)
+        nc.vector.tensor_copy(
+            out=m.rearrange("p (a e) (u q) -> p a e u q", e=2, u=ROWS)[:, :, 1, :, :],
+            in_=adj_rows[:].rearrange("p (a e) (q u) -> p a e u q", e=2, u=ROWS)[:, :, 1, :, :],
+        )
+        root = keep.tile([P, ROWS], F32)
+        nc.scalar.activation(
+            out=root[:].rearrange("p (a e) -> p a e", a=2),
+            in_=sums[:].rearrange("p (a e) -> p a e", a=2)[:, :, 0:2],
+            func=ACT.Sqrt,
+            bias=1.0,
+            scale=1.0,
+        )
+        dd = keep.tile([P, ROWS], F32)
+        nc.vector.reciprocal(out=dd[:], in_=root[:])
+        squares = m_flat[:].rearrange("p (t w) -> p t w", w=pitch)[:, :, 0:P]
+        nc.vector.tensor_tensor(
+            out=squares,
+            in0=squares,
+            in1=identity[:].unsqueeze(1).to_broadcast([P, ROWS, P]),
+            op=ALU.add,
+        )
+        dd_cols = psum_x2.tile([P, NODES], F32, tag="x2")
+        for u in range(ROWS):
             nc.tensor.transpose(
-                out=drow[:, u * P : (u + 1) * P],
-                in_=dcol[:, c : c + 1].to_broadcast([P, P]),
-                identity=ident[:],
+                out=dd_cols[:, u * P : (u + 1) * P],
+                in_=dd[:, dd_at[u] : dd_at[u] + 1].to_broadcast([P, P]),
+                identity=identity[:],
             )
-
-        def t1_op(t):
-            c = SUM_COL[t]
+        scaled = keep.tile([P, ROWS, NODES], F32)
+        for t in range(ROWS):
             nc.vector.tensor_scalar(
-                out=t1[:, t, :], in0=mfp[:, t, :], scalar1=dcol[:, c : c + 1], scalar2=None, op0=ALU.mult
+                out=scaled[:, t, :],
+                in0=m[:, t, :],
+                scalar1=dd[:, dd_at[t] : dd_at[t] + 1],
+                scalar2=None,
+                op0=ALU.mult,
+            )
+        s_grouped = keep.tile([P, NODES, ROWS], BF16, align_bytes=64)
+        s_codes = keep.tile([P, NODES], U32, align_bytes=64)
+        s_scales = keep.tile([P, NODES], U8, align_bytes=64)
+
+        def quantise_s(u):
+            cols = slice(u * P, (u + 1) * P)
+            nc.vector.quantize_mx(
+                out=s_codes[:, cols].bitcast(FP8X4),
+                scales=s_scales[:, cols],
+                in_=s_grouped[:, cols, :].rearrange("p q t -> p (q t)"),
             )
 
-        def gp(u):
+        for u in range(ROWS):
             cols = slice(u * P, (u + 1) * P)
             nc.vector.tensor_tensor(
-                out=gs[:, cols, :],
-                in0=t1[:, :, cols].rearrange("p t q -> p q t"),
-                in1=drow[:, cols].unsqueeze(2).to_broadcast([P, P, PACK]),
+                out=s_grouped[:, cols, :],
+                in0=scaled[:, :, cols].rearrange("p t q -> p q t"),
+                in1=dd_cols[:, cols].unsqueeze(2).to_broadcast([P, P, ROWS]),
                 op=ALU.mult,
             )
+            if u > 0:
+                quantise_s(u - 1)
+        quantise_s(ROWS - 1)
 
-        def qs(u):
-            cols = slice(u * P, (u + 1) * P)
+        def swap_axes(on_scalar, rows_first, kind, n):
+            tile = grouped.tile([P, BLOCK, ROWS], BF16, name="%s_%d" % (kind, n), tag=kind, align_bytes=64)
+            out, in_ = by_fours(rows_first, tile[:])
+            if on_scalar:
+                nc.scalar.copy(out=out, in_=in_)
+            else:
+                nc.vector.tensor_copy(out=out, in_=in_)
+            return tile
+
+        def quantise(tile, kind, n):
+            codes = packed.tile([P, BLOCK], U32, name="%s_codes_%d" % (kind, n), tag=kind + "_codes", align_bytes=64)
+            scales = packed.tile([P, BLOCK], U8, name="%s_scales_%d" % (kind, n), tag=kind + "_scales", align_bytes=64)
             nc.vector.quantize_mx(
-                out=sc[:, cols].bitcast(FP8X4),
-                scales=ss[:, cols],
-                in_=gs[:, cols, :].rearrange("p q t -> p (q t)"),
+                out=codes[:].bitcast(FP8X4), scales=scales[:], in_=tile[:].rearrange("p f t -> p (f t)")
             )
+            return codes, scales
 
-        def regroup(n, eng_copy):
-            b, f0 = where(n)
-            g = stage.tile([P, BLK, PACK], BF16, name="g0_%d" % n, tag="g0", align_bytes=64)
-            eng_copy(
-                out=g[:].rearrange("p (c i) t -> p c t i", i=4),
-                in_=xr[b][:, :, f0 : f0 + BLK].rearrange("p t (c i) -> p c t i", i=4),
-            )
-            g0[n] = g
-
-        def interleave(n, eng_copy):
-            b, f0 = where(n)
-            g = stage.tile([P, BLK, PACK], BF16, name="g1_%d" % n, tag="g1", align_bytes=64)
-            eng_copy(
-                out=g[:].rearrange("p (c i) t -> p c t i", i=4),
-                in_=x1f[b][:, :, f0 : f0 + BLK].rearrange("p t (c i) -> p c t i", i=4),
-            )
-            g1[n] = g
-
-        def quant(n, grouped, cdict, sdict, kind):
-            c = codes.tile([P, BLK], U32, name="c%s_%d" % (kind, n), tag="c" + kind, align_bytes=64)
-            s = codes.tile([P, BLK], U8, name="s%s_%d" % (kind, n), tag="s" + kind, align_bytes=64)
-            nc.vector.quantize_mx(
-                out=c[:].bitcast(FP8X4), scales=s[:], in_=grouped[n][:].rearrange("p f t -> p (f t)")
-            )
-            cdict[n] = c
-            sdict[n] = s
-
-        def mm(k, pool, tag, cdict, sdict, banks):
-            b, v, j = bank_of(k)
-            n = b * PER_BATCH + j
-            bank = pool.tile([P, 2, BLK], F32, name="%s_%d" % (tag, k), tag=tag)
+        def multiply(pool, kind, pair, operand):
+            codes, scales = operand
+            bank = pool.tile([P, 2, BLOCK], F32, name=kind, tag=kind)
             for w in range(2):
-                u = 2 * v + w
-                rows = slice(u * P, (u + 1) * P)
+                cols = slice((2 * pair + w) * P, (2 * pair + w + 1) * P)
                 nc.tensor.matmul_mx(
                     out=bank[:, w, :],
-                    lhsT=sc[:, rows].bitcast(FP8X4),
-                    lhsT_scale=ss[:, rows],
-                    rhs=cdict[n][:].bitcast(FP8X4),
-                    rhs_scale=sdict[n][:],
+                    lhsT=s_codes[:, cols].bitcast(FP8X4),
+                    lhsT_scale=s_scales[:, cols],
+                    rhs=codes[:].bitcast(FP8X4),
+                    rhs_scale=scales[:],
                     start=True,
                     stop=True,
                 )
-            banks[k] = bank
+            return bank
 
-        def e1(k):
-            b, v, j = bank_of(k)
-            if v == 0 and j == 0:
-                x1f[b] = outs.tile([P, PACK, FEAT], F32, name="x1f%d" % b, tag="x1f")
-            nc.scalar.copy(
-                out=x1f[b][:, 2 * v : 2 * v + 2, j * BLK : (j + 1) * BLK], in_=p1[k][:]
-            )
+        def block_slice(tile, pair_rows, j):
+            return tile[:, pair_rows, j * BLOCK : (j + 1) * BLOCK]
 
-        def e2(k):
-            b, v, j = bank_of(k)
-            if v == 0 and j == 0:
-                x2f[b] = outs.tile([P, PACK, FEAT], F32, name="x2f%d" % b, tag="x2f")
-            nc.vector.scalar_tensor_tensor(
-                out=x2f[b][:, 2 * v : 2 * v + 2, j * BLK : (j + 1) * BLK],
-                in0=p2[k][:],
-                scalar=2.0,
-                in1=xr[b][:, 2 * v : 2 * v + 2, j * BLK : (j + 1) * BLK],
-                op0=ALU.mult,
-                op1=ALU.subtract,
-            )
-
-        def store(dram, sb, h):
-            b, v = divmod(h, 2)
+        def store_pair(dram, tile, b, pair_rows):
             nc.sync.dma_start(
-                out=dram[b].rearrange("(p t) f -> p t f", t=PACK)[:, 2 * v : 2 * v + 2, :],
-                in_=sb[b][:, 2 * v : 2 * v + 2, :],
+                out=dram[b].rearrange("(p t) f -> p t f", t=ROWS)[:, pair_rows, :], in_=tile[:, pair_rows, :]
             )
 
-        ops = {
-            "ld_a": ld_a,
-            "ld_x": ld_x,
-            "act": act,
-            "red": red,
-            "cast": cast,
-            "sqrt": sqrt,
-            "diag": diag,
-            "recip": recip,
-            "tr": tr,
-            "t1": t1_op,
-            "gp": gp,
-            "qs": qs,
-            "rgS": lambda n: regroup(n, nc.scalar.copy),
-            "rgV": lambda n: regroup(n, nc.vector.tensor_copy),
-            "ilS": lambda n: interleave(n, nc.scalar.copy),
-            "ilV": lambda n: interleave(n, nc.vector.tensor_copy),
-            "q0": lambda n: quant(n, g0, c0, s0, "0"),
-            "q1": lambda n: quant(n, g1, c1, s1, "1"),
-            "mm1": lambda k: mm(k, ps1, "p1", c0, s0, p1),
-            "mm2": lambda k: mm(k, ps2, "p2", c1, s1, p2),
-            "e1": e1,
-            "e2": e2,
-            "st1": lambda h: store(out_0, x1f, h),
-            "st2": lambda h: store(out_1, x2f, h),
-        }
-        for name, arg in ORDER:
-            ops[name](arg)
+        x0_grouped = []
+        x0_packed = []
+        for n in range(N_BLOCKS):
+            b, j = divmod(n, BLOCKS_PER_BATCH)
+            x0_grouped.append(swap_axes(n < SCALAR_REGROUPS, block_slice(x0[b], slice(0, ROWS), j), "x0g", n))
+            if n > 0:
+                x0_packed.append(quantise(x0_grouped[n - 1], "x0", n - 1))
+        x0_packed.append(quantise(x0_grouped[N_BLOCKS - 1], "x0", N_BLOCKS - 1))
+
+        x1 = []
+        for b in range(BATCH):
+            x1_b = results.tile([P, ROWS, FEAT], F32, name="x1_%d" % b, tag="x1")
+            x1.append(x1_b)
+            for pair in range(PAIRS):
+                pair_rows = slice(2 * pair, 2 * pair + 2)
+                for j in range(BLOCKS_PER_BATCH):
+                    bank = multiply(psum_x1, "x1", pair, x0_packed[b * BLOCKS_PER_BATCH + j])
+                    nc.scalar.copy(out=block_slice(x1_b, pair_rows, j), in_=bank[:])
+                store_pair(out_0, x1_b, b, pair_rows)
+
+        x1_packed = []
+
+        def prepare(b):
+            tiles = []
+            for j in range(BLOCKS_PER_BATCH):
+                n = b * BLOCKS_PER_BATCH + j
+                tiles.append(swap_axes(n >= VECTOR_INTERLEAVES, block_slice(x1[b], slice(0, ROWS), j), "x1g", n))
+                if j > 0:
+                    x1_packed.append(quantise(tiles[j - 1], "x1", n - 1))
+            x1_packed.append(quantise(tiles[BLOCKS_PER_BATCH - 1], "x1", n))
+
+        prepare(0)
+        for b in range(BATCH):
+            if b + 1 < BATCH:
+                prepare(b + 1)
+            x2_b = results.tile([P, ROWS, FEAT], F32, name="x2_%d" % b, tag="x2")
+            for pair in range(PAIRS):
+                pair_rows = slice(2 * pair, 2 * pair + 2)
+                for j in range(BLOCKS_PER_BATCH):
+                    bank = multiply(psum_x2, "x2", pair, x1_packed[b * BLOCKS_PER_BATCH + j])
+                    nc.vector.scalar_tensor_tensor(
+                        out=block_slice(x2_b, pair_rows, j),
+                        in0=bank[:],
+                        scalar=2.0,
+                        in1=block_slice(x0[b], pair_rows, j),
+                        op0=ALU.mult,
+                        op1=ALU.subtract,
+                    )
+                store_pair(out_1, x2_b, b, pair_rows)

@@ -72,19 +72,14 @@ def tile_dgcn_pa_kernel(tc, inputs, adj, out_0, out_1):
         dd_at = {1: 0, 3: 1, 0: 2, 2: 3}
         for t in range(ROWS):
             total = sums[:, sum_at[t] : sum_at[t] + 1]
+            as_f32 = m[:, t, :].rearrange("p (u q) -> p u q", u=ROWS)
+            row = adj_rows[:, t, :].rearrange("p (q u) -> p u q", u=ROWS)
             if t % 2 == 0:
-                nc.scalar.activation(
-                    out=m[:, t, :].rearrange("p (u q) -> p u q", u=ROWS),
-                    in_=adj_rows[:, t, :].rearrange("p (q u) -> p u q", u=ROWS),
-                    func=ACT.Copy,
-                    accum_out=total,
-                )
+                nc.scalar.activation(out=as_f32, in_=row, func=ACT.Copy, accum_out=total)
             else:
-                nc.vector.tensor_reduce(out=total, in_=adj_rows[:, t, :], axis=AX.X, op=ALU.add)
-        nc.vector.tensor_copy(
-            out=m.rearrange("p (a e) (u q) -> p a e u q", e=2, u=ROWS)[:, :, 1, :, :],
-            in_=adj_rows[:].rearrange("p (a e) (q u) -> p a e u q", e=2, u=ROWS)[:, :, 1, :, :],
-        )
+                nc.vector.tensor_scalar(
+                    out=as_f32, in0=row, scalar1=1.0, scalar2=None, op0=ALU.mult, op1=ALU.add, accum_out=total
+                )
         root = keep.tile([P, ROWS], F32)
         nc.scalar.activation(
             out=root[:].rearrange("p (a e) -> p a e", a=2),
@@ -93,8 +88,6 @@ def tile_dgcn_pa_kernel(tc, inputs, adj, out_0, out_1):
             bias=1.0,
             scale=1.0,
         )
-        dd = keep.tile([P, ROWS], F32)
-        nc.vector.reciprocal(out=dd[:], in_=root[:])
         squares = m_flat[:].rearrange("p (t w) -> p t w", w=pitch)[:, :, 0:P]
         nc.vector.tensor_tensor(
             out=squares,
@@ -102,6 +95,8 @@ def tile_dgcn_pa_kernel(tc, inputs, adj, out_0, out_1):
             in1=identity[:].unsqueeze(1).to_broadcast([P, ROWS, P]),
             op=ALU.add,
         )
+        dd = keep.tile([P, ROWS], F32)
+        nc.vector.reciprocal(out=dd[:], in_=root[:])
         dd_cols = psum_x2.tile([P, NODES], F32, tag="x2")
         for u in range(ROWS):
             nc.tensor.transpose(

@@ -10,7 +10,6 @@ U32 = mybir.dt.uint32
 U8 = mybir.dt.uint8
 ALU = mybir.AluOpType
 ACT = mybir.ActivationFunctionType
-AX = mybir.AxisListType
 
 P = 128
 ROWS = 4
@@ -21,10 +20,9 @@ BLOCK = 256
 BLOCKS_PER_BATCH = FEAT // BLOCK
 N_BLOCKS = BATCH * BLOCKS_PER_BATCH
 PAIRS = ROWS // 2
-BANKS_PER_BATCH = PAIRS * BLOCKS_PER_BATCH
+UNITS = BATCH * PAIRS
 
 SCALAR_REGROUPS = 5
-VECTOR_INTERLEAVES = 7
 
 FLOPS = 2 * 2 * BATCH * NODES * NODES * FEAT
 
@@ -43,6 +41,7 @@ def tile_dgcn_pa_kernel(tc, inputs, adj, out_0, out_1):
         grouped = ctx.enter_context(tc.tile_pool(name="grouped", bufs=2 * BLOCKS_PER_BATCH))
         packed = ctx.enter_context(tc.tile_pool(name="packed", bufs=N_BLOCKS))
         results = ctx.enter_context(tc.tile_pool(name="results", bufs=BATCH))
+        handoff = ctx.enter_context(tc.tile_pool(name="handoff", bufs=1))
         psum_x1 = ctx.enter_context(tc.psum_pool(name="psum_x1", bufs=4))
         psum_x2 = ctx.enter_context(tc.psum_pool(name="psum_x2", bufs=4))
         ctx.enter_context(tc.manual_schedule())
@@ -63,6 +62,37 @@ def tile_dgcn_pa_kernel(tc, inputs, adj, out_0, out_1):
         nc.vector.memset(ones[:], 1.0)
         dummy = keep.tile([P, 8], F32)
         nc.scalar.activation(out=dummy[:], in_=ones[:], func=ACT.Sqrt)
+
+        def block_slice(tile, rows, j):
+            return tile[:, rows, j * BLOCK : (j + 1) * BLOCK]
+
+        def swap_axes(on_scalar, rows_first, kind, n):
+            tile = grouped.tile([P, BLOCK, ROWS], BF16, name="%s_%d" % (kind, n), tag=kind, align_bytes=64)
+            out, in_ = by_fours(rows_first, tile[:])
+            if on_scalar:
+                nc.scalar.copy(out=out, in_=in_)
+            else:
+                nc.vector.tensor_copy(out=out, in_=in_)
+            return tile
+
+        def quantise(tile, kind, n):
+            codes = packed.tile([P, BLOCK], U32, name="%s_codes_%d" % (kind, n), tag=kind + "_codes", align_bytes=64)
+            scales = packed.tile([P, BLOCK], U8, name="%s_scales_%d" % (kind, n), tag=kind + "_scales", align_bytes=64)
+            nc.vector.quantize_mx(
+                out=codes[:].bitcast(FP8X4), scales=scales[:], in_=tile[:].rearrange("p f t -> p (f t)")
+            )
+            return codes, scales
+
+        x0_grouped = {}
+        x0_packed = {}
+
+        def regroup_x0(n):
+            b, j = divmod(n, BLOCKS_PER_BATCH)
+            rows_first = block_slice(x0[b], slice(0, ROWS), j)
+            x0_grouped[n] = swap_axes(n < SCALAR_REGROUPS, rows_first, "x0g", n)
+
+        def quantise_x0(n):
+            x0_packed[n] = quantise(x0_grouped[n], "x0", n)
 
         pitch = NODES + P
         m_flat = keep.tile([P, ROWS * pitch], F32)
@@ -104,6 +134,8 @@ def tile_dgcn_pa_kernel(tc, inputs, adj, out_0, out_1):
                 in_=dd[:, dd_at[u] : dd_at[u] + 1].to_broadcast([P, P]),
                 identity=identity[:],
             )
+        for n in range(SCALAR_REGROUPS):
+            regroup_x0(n)
         scaled = keep.tile([P, ROWS, NODES], F32)
         for t in range(ROWS):
             nc.vector.tensor_scalar(
@@ -117,6 +149,15 @@ def tile_dgcn_pa_kernel(tc, inputs, adj, out_0, out_1):
         s_codes = keep.tile([P, NODES], U32, align_bytes=64)
         s_scales = keep.tile([P, NODES], U8, align_bytes=64)
 
+        def scale_s(u):
+            cols = slice(u * P, (u + 1) * P)
+            nc.vector.tensor_tensor(
+                out=s_grouped[:, cols, :],
+                in0=scaled[:, :, cols].rearrange("p t q -> p q t"),
+                in1=dd_cols[:, cols].unsqueeze(2).to_broadcast([P, P, ROWS]),
+                op=ALU.mult,
+            )
+
         def quantise_s(u):
             cols = slice(u * P, (u + 1) * P)
             nc.vector.quantize_mx(
@@ -125,34 +166,14 @@ def tile_dgcn_pa_kernel(tc, inputs, adj, out_0, out_1):
                 in_=s_grouped[:, cols, :].rearrange("p q t -> p (q t)"),
             )
 
-        for u in range(ROWS):
-            cols = slice(u * P, (u + 1) * P)
-            nc.vector.tensor_tensor(
-                out=s_grouped[:, cols, :],
-                in0=scaled[:, :, cols].rearrange("p t q -> p q t"),
-                in1=dd_cols[:, cols].unsqueeze(2).to_broadcast([P, P, ROWS]),
-                op=ALU.mult,
-            )
-            if u > 0:
-                quantise_s(u - 1)
-        quantise_s(ROWS - 1)
-
-        def swap_axes(on_scalar, rows_first, kind, n):
-            tile = grouped.tile([P, BLOCK, ROWS], BF16, name="%s_%d" % (kind, n), tag=kind, align_bytes=64)
-            out, in_ = by_fours(rows_first, tile[:])
-            if on_scalar:
-                nc.scalar.copy(out=out, in_=in_)
-            else:
-                nc.vector.tensor_copy(out=out, in_=in_)
-            return tile
-
-        def quantise(tile, kind, n):
-            codes = packed.tile([P, BLOCK], U32, name="%s_codes_%d" % (kind, n), tag=kind + "_codes", align_bytes=64)
-            scales = packed.tile([P, BLOCK], U8, name="%s_scales_%d" % (kind, n), tag=kind + "_scales", align_bytes=64)
-            nc.vector.quantize_mx(
-                out=codes[:].bitcast(FP8X4), scales=scales[:], in_=tile[:].rearrange("p f t -> p (f t)")
-            )
-            return codes, scales
+        scale_s(0)
+        scale_s(1)
+        quantise_s(0)
+        scale_s(2)
+        quantise_s(1)
+        scale_s(3)
+        quantise_s(2)
+        quantise_s(3)
 
         def multiply(pool, kind, pair, operand):
             codes, scales = operand
@@ -170,60 +191,103 @@ def tile_dgcn_pa_kernel(tc, inputs, adj, out_0, out_1):
                 )
             return bank
 
-        def block_slice(tile, pair_rows, j):
-            return tile[:, pair_rows, j * BLOCK : (j + 1) * BLOCK]
-
         def store_pair(dram, tile, b, pair_rows):
             nc.sync.dma_start(
                 out=dram[b].rearrange("(p t) f -> p t f", t=ROWS)[:, pair_rows, :], in_=tile[:, pair_rows, :]
             )
 
-        x0_grouped = []
-        x0_packed = []
+        x1 = [results.tile([P, ROWS, FEAT], F32, name="x1_%d" % b, tag="x1") for b in range(BATCH)]
+        x2 = [results.tile([P, ROWS, FEAT], F32, name="x2_%d" % b, tag="x2") for b in range(BATCH)]
+        x1_grouped = {}
+        x1_packed = {}
+
+        def bank_x1(unit, j):
+            b, pair = divmod(unit, PAIRS)
+            bank = multiply(psum_x1, "x1", pair, x0_packed[b * BLOCKS_PER_BATCH + j])
+            nc.scalar.copy(out=block_slice(x1[b], slice(2 * pair, 2 * pair + 2), j), in_=bank[:])
+
+        def bank_x2(unit, j):
+            b, pair = divmod(unit, PAIRS)
+            pair_rows = slice(2 * pair, 2 * pair + 2)
+            bank = multiply(psum_x2, "x2", pair, x1_packed[b * BLOCKS_PER_BATCH + j])
+            nc.vector.scalar_tensor_tensor(
+                out=block_slice(x2[b], pair_rows, j),
+                in0=bank[:],
+                scalar=2.0,
+                in1=block_slice(x0[b], pair_rows, j),
+                op0=ALU.mult,
+                op1=ALU.subtract,
+            )
+
+        def store_unit(dram, tiles, unit):
+            b, pair = divmod(unit, PAIRS)
+            store_pair(dram, tiles[b], b, slice(2 * pair, 2 * pair + 2))
+
+        def interleave_x1(b, j):
+            n = b * BLOCKS_PER_BATCH + j
+            rows_first = block_slice(x1[b], slice(0, ROWS), j)
+            if j == 2:
+                x1_grouped[n] = swap_axes(b > 0, rows_first, "x1g", n)
+                return
+            tile = handoff.tile([P, BLOCK, ROWS], BF16, name="x1h_%d" % n, tag="x1h_%d" % j, align_bytes=64)
+            x1_grouped[n] = tile
+            if b == 0:
+                out, in_ = by_fours(rows_first, tile[:])
+                nc.vector.tensor_copy(out=out, in_=in_)
+            else:
+                nc.gpsimd.tensor_scalar(
+                    out=tile[:],
+                    in0=rows_first.rearrange("p t c -> p c t"),
+                    scalar1=1.0,
+                    scalar2=0.0,
+                    op0=ALU.mult,
+                    op1=ALU.add,
+                )
+
+        def quantise_x1(b, j):
+            n = b * BLOCKS_PER_BATCH + j
+            x1_packed[n] = quantise(x1_grouped[n], "x1", n)
+
         for n in range(N_BLOCKS):
-            b, j = divmod(n, BLOCKS_PER_BATCH)
-            x0_grouped.append(swap_axes(n < SCALAR_REGROUPS, block_slice(x0[b], slice(0, ROWS), j), "x0g", n))
+            if n >= SCALAR_REGROUPS:
+                regroup_x0(n)
             if n > 0:
-                x0_packed.append(quantise(x0_grouped[n - 1], "x0", n - 1))
-        x0_packed.append(quantise(x0_grouped[N_BLOCKS - 1], "x0", N_BLOCKS - 1))
+                quantise_x0(n - 1)
+        quantise_x0(N_BLOCKS - 1)
 
-        x1 = []
-        for b in range(BATCH):
-            x1_b = results.tile([P, ROWS, FEAT], F32, name="x1_%d" % b, tag="x1")
-            x1.append(x1_b)
-            for pair in range(PAIRS):
-                pair_rows = slice(2 * pair, 2 * pair + 2)
-                for j in range(BLOCKS_PER_BATCH):
-                    bank = multiply(psum_x1, "x1", pair, x0_packed[b * BLOCKS_PER_BATCH + j])
-                    nc.scalar.copy(out=block_slice(x1_b, pair_rows, j), in_=bank[:])
-                store_pair(out_0, x1_b, b, pair_rows)
+        ORDER = (1, 2, 0)
 
-        x1_packed = []
-
-        def prepare(b):
-            tiles = []
+        def unit_x1(unit):
             for j in range(BLOCKS_PER_BATCH):
-                n = b * BLOCKS_PER_BATCH + j
-                tiles.append(swap_axes(n >= VECTOR_INTERLEAVES, block_slice(x1[b], slice(0, ROWS), j), "x1g", n))
-                if j > 0:
-                    x1_packed.append(quantise(tiles[j - 1], "x1", n - 1))
-            x1_packed.append(quantise(tiles[BLOCKS_PER_BATCH - 1], "x1", n))
+                bank_x1(unit, j)
+            store_unit(out_0, x1, unit)
 
-        prepare(0)
+        EARLY = UNITS - PAIRS
+        for unit in range(EARLY):
+            unit_x1(unit)
+            if unit >= 4 and unit % PAIRS == 0:
+                interleave_x1(unit // PAIRS - 1, 2)
+        interleave_x1(0, 1)
+        interleave_x1(0, 2)
+        quantise_x1(0, 1)
+        interleave_x1(0, 0)
+        quantise_x1(0, 2)
+        quantise_x1(0, 0)
         for b in range(BATCH):
             if b + 1 < BATCH:
-                prepare(b + 1)
-            x2_b = results.tile([P, ROWS, FEAT], F32, name="x2_%d" % b, tag="x2")
+                interleave_x1(b + 1, 0)
+                interleave_x1(b + 1, 1)
             for pair in range(PAIRS):
-                pair_rows = slice(2 * pair, 2 * pair + 2)
-                for j in range(BLOCKS_PER_BATCH):
-                    bank = multiply(psum_x2, "x2", pair, x1_packed[b * BLOCKS_PER_BATCH + j])
-                    nc.vector.scalar_tensor_tensor(
-                        out=block_slice(x2_b, pair_rows, j),
-                        in0=bank[:],
-                        scalar=2.0,
-                        in1=block_slice(x0[b], pair_rows, j),
-                        op0=ALU.mult,
-                        op1=ALU.subtract,
-                    )
-                store_pair(out_1, x2_b, b, pair_rows)
+                for j in ORDER:
+                    bank_x2(b * PAIRS + pair, j)
+                    if b == 0:
+                        bank_x1(EARLY + pair, j)
+                store_unit(out_1, x2, b * PAIRS + pair)
+                if b == 0:
+                    store_unit(out_0, x1, EARLY + pair)
+            if b == 0:
+                interleave_x1(2, 2)
+                interleave_x1(3, 2)
+            if b + 1 < BATCH:
+                for j in ORDER:
+                    quantise_x1(b + 1, j)

@@ -22,7 +22,7 @@ N_BLOCKS = BATCH * BLOCKS_PER_BATCH
 PAIRS = ROWS // 2
 UNITS = BATCH * PAIRS
 
-SCALAR_REGROUPS = 5
+SCALAR_REGROUPS = 3
 
 FLOPS = 2 * 2 * BATCH * NODES * NODES * FEAT
 
@@ -171,8 +171,12 @@ def tile_dgcn_pa_kernel(tc, inputs, adj, out_0, out_1):
         quantise_s(0)
         scale_s(2)
         quantise_s(1)
+        quantise_x0(0)
+        quantise_x0(1)
+        quantise_x0(2)
         scale_s(3)
         quantise_s(2)
+        regroup_x0(3)
         quantise_s(3)
 
         def multiply(pool, kind, pair, operand):
@@ -248,11 +252,9 @@ def tile_dgcn_pa_kernel(tc, inputs, adj, out_0, out_1):
             n = b * BLOCKS_PER_BATCH + j
             x1_packed[n] = quantise(x1_grouped[n], "x1", n)
 
-        for n in range(N_BLOCKS):
-            if n >= SCALAR_REGROUPS:
-                regroup_x0(n)
-            if n > 0:
-                quantise_x0(n - 1)
+        for n in range(4, N_BLOCKS):
+            regroup_x0(n)
+            quantise_x0(n - 1)
         quantise_x0(N_BLOCKS - 1)
 
         ORDER = (1, 2, 0)

@@ -46,13 +46,13 @@ def tile_dgcn_pa_kernel(tc, inputs, adj, out_0, out_1):
         psum_x2 = ctx.enter_context(tc.psum_pool(name="psum_x2", bufs=4))
         ctx.enter_context(tc.manual_schedule())
 
-        adj_rows = keep.tile([P, ROWS, NODES], BF16)
+        adj_rows = keep.tile([P, ROWS, NODES], BF16, align_bytes=256)
         adj_view = adj.rearrange("(p t) i -> p t i", t=ROWS)
         for t in range(ROWS):
             nc.sync.dma_start(out=adj_rows[:, t, :], in_=adj_view[:, t, :])
         x0 = []
         for b in range(BATCH):
-            x0_b = keep.tile([P, ROWS, FEAT], BF16, name="x0_%d" % b)
+            x0_b = keep.tile([P, ROWS, FEAT], BF16, name="x0_%d" % b, align_bytes=256)
             nc.sync.dma_start(out=x0_b[:], in_=inputs[b].rearrange("(p t) f -> p t f", t=ROWS))
             x0.append(x0_b)
 
@@ -200,8 +200,8 @@ def tile_dgcn_pa_kernel(tc, inputs, adj, out_0, out_1):
                 out=dram[b].rearrange("(p t) f -> p t f", t=ROWS)[:, pair_rows, :], in_=tile[:, pair_rows, :]
             )
 
-        x1 = [results.tile([P, ROWS, FEAT], F32, name="x1_%d" % b, tag="x1") for b in range(BATCH)]
-        x2 = [results.tile([P, ROWS, FEAT], F32, name="x2_%d" % b, tag="x2") for b in range(BATCH)]
+        x1 = [results.tile([P, ROWS, FEAT], F32, name="x1_%d" % b, tag="x1", align_bytes=256) for b in range(BATCH)]
+        x2 = [results.tile([P, ROWS, FEAT], F32, name="x2_%d" % b, tag="x2", align_bytes=256) for b in range(BATCH)]
         x1_grouped = {}
         x1_packed = {}
 

@@ -20,9 +20,13 @@ BLOCK = 256
 BLOCKS_PER_BATCH = FEAT // BLOCK
 N_BLOCKS = BATCH * BLOCKS_PER_BATCH
 PAIRS = ROWS // 2
+GROUPED = 6
+BANKS = 4
 UNITS = BATCH * PAIRS
 
 SCALAR_REGROUPS = 3
+EARLY_BATCHES = 3
+EARLY_BLOCKS = EARLY_BATCHES * BLOCKS_PER_BATCH
 
 FLOPS = 2 * 2 * BATCH * NODES * NODES * FEAT
 
@@ -38,12 +42,12 @@ def tile_dgcn_pa_kernel(tc, inputs, adj, out_0, out_1):
     nc = tc.nc
     with ExitStack() as ctx:
         keep = ctx.enter_context(tc.tile_pool(name="keep", bufs=1))
-        grouped = ctx.enter_context(tc.tile_pool(name="grouped", bufs=2 * BLOCKS_PER_BATCH))
+        grouped = ctx.enter_context(tc.tile_pool(name="grouped", bufs=GROUPED))
         packed = ctx.enter_context(tc.tile_pool(name="packed", bufs=N_BLOCKS))
         results = ctx.enter_context(tc.tile_pool(name="results", bufs=BATCH))
         handoff = ctx.enter_context(tc.tile_pool(name="handoff", bufs=1))
-        psum_x1 = ctx.enter_context(tc.psum_pool(name="psum_x1", bufs=4))
-        psum_x2 = ctx.enter_context(tc.psum_pool(name="psum_x2", bufs=4))
+        psum_x1 = ctx.enter_context(tc.psum_pool(name="psum_x1", bufs=BANKS))
+        psum_x2 = ctx.enter_context(tc.psum_pool(name="psum_x2", bufs=BANKS))
         ctx.enter_context(tc.manual_schedule())
 
         adj_rows = keep.tile([P, ROWS, NODES], BF16, align_bytes=256)
@@ -56,24 +60,34 @@ def tile_dgcn_pa_kernel(tc, inputs, adj, out_0, out_1):
             nc.sync.dma_start(out=x0_b[:], in_=inputs[b].rearrange("(p t) f -> p t f", t=ROWS))
             x0.append(x0_b)
 
-        identity = keep.tile([P, P], F32)
-        make_identity(nc, identity[:])
+        unit = keep.tile([P, (2 * ROWS - 2) * P], F32)
+        nc.gpsimd.memset(unit[:], 0.0)
+        identity = unit[:, (ROWS - 1) * P : ROWS * P]
+        make_identity(nc, identity)
         ones = keep.tile([P, 8], F32)
         nc.vector.memset(ones[:], 1.0)
         dummy = keep.tile([P, 8], F32)
-        nc.scalar.activation(out=dummy[:], in_=ones[:], func=ACT.Sqrt)
+        nc.scalar.activation(out=dummy[:], in_=ones[:], func=ACT.Abs_reciprocal_sqrt)
 
         def block_slice(tile, rows, j):
             return tile[:, rows, j * BLOCK : (j + 1) * BLOCK]
 
-        def swap_axes(on_scalar, rows_first, kind, n):
-            tile = grouped.tile([P, BLOCK, ROWS], BF16, name="%s_%d" % (kind, n), tag=kind, align_bytes=64)
+        def swap_axes(engine, rows_first, tile):
+            if engine == "gpsimd":
+                nc.gpsimd.tensor_scalar(
+                    out=tile[:],
+                    in0=rows_first.rearrange("p t c -> p c t"),
+                    scalar1=1.0,
+                    scalar2=0.0,
+                    op0=ALU.mult,
+                    op1=ALU.add,
+                )
+                return
             out, in_ = by_fours(rows_first, tile[:])
-            if on_scalar:
+            if engine == "scalar":
                 nc.scalar.copy(out=out, in_=in_)
             else:
                 nc.vector.tensor_copy(out=out, in_=in_)
-            return tile
 
         def quantise(tile, kind, n):
             codes = packed.tile([P, BLOCK], U32, name="%s_codes_%d" % (kind, n), tag=kind + "_codes", align_bytes=64)
@@ -86,65 +100,69 @@ def tile_dgcn_pa_kernel(tc, inputs, adj, out_0, out_1):
         x0_grouped = {}
         x0_packed = {}
 
-        def regroup_x0(n):
+        def regroup_x0(engine, n):
             b, j = divmod(n, BLOCKS_PER_BATCH)
-            rows_first = block_slice(x0[b], slice(0, ROWS), j)
-            x0_grouped[n] = swap_axes(n < SCALAR_REGROUPS, rows_first, "x0g", n)
+            x0_grouped[n] = grouped.tile([P, BLOCK, ROWS], BF16, name="x0g_%d" % n, tag="x0g", align_bytes=64)
+            swap_axes(engine, block_slice(x0[b], slice(0, ROWS), j), x0_grouped[n])
 
         def quantise_x0(n):
             x0_packed[n] = quantise(x0_grouped[n], "x0", n)
 
-        pitch = NODES + P
-        m_flat = keep.tile([P, ROWS * pitch], F32)
+        pitch = 2 * NODES + 2 * P
+        m_flat = keep.tile([P, 2 * pitch], F32)
         m = m_flat[:, 0 : ROWS * NODES].rearrange("p (t c) -> p t c", t=ROWS)
         sums = keep.tile([P, 16], F32)
+        SCALAR_ROWS = slice(0, ROWS, 2)
+        VECTOR_ROWS = slice(1, ROWS, 2)
         sum_at = {1: 0, 3: 1, 0: 8, 2: 9}
-        dd_at = {1: 0, 3: 1, 0: 2, 2: 3}
-        for t in range(ROWS):
+        dd = keep.tile([P, ROWS], F32)
+
+        def to_f32(t):
             total = sums[:, sum_at[t] : sum_at[t] + 1]
             as_f32 = m[:, t, :].rearrange("p (u q) -> p u q", u=ROWS)
             row = adj_rows[:, t, :].rearrange("p (q u) -> p u q", u=ROWS)
             if t % 2 == 0:
                 nc.scalar.activation(out=as_f32, in_=row, func=ACT.Copy, accum_out=total)
             else:
-                nc.vector.tensor_scalar(
-                    out=as_f32, in0=row, scalar1=1.0, scalar2=None, op0=ALU.mult, op1=ALU.add, accum_out=total
+                window = unit[:, (ROWS - 1 - t) * P : (ROWS - 1 - t) * P + NODES]
+                nc.vector.scalar_tensor_tensor(
+                    out=as_f32,
+                    in0=row,
+                    scalar=1.0,
+                    in1=window.rearrange("p (u q) -> p u q", u=ROWS),
+                    op0=ALU.mult,
+                    op1=ALU.add,
+                    accum_out=total,
                 )
-        root = keep.tile([P, ROWS], F32)
-        nc.scalar.activation(
-            out=root[:].rearrange("p (a e) -> p a e", a=2),
-            in_=sums[:].rearrange("p (a e) -> p a e", a=2)[:, :, 0:2],
-            func=ACT.Sqrt,
-            bias=1.0,
-            scale=1.0,
-        )
-        squares = m_flat[:].rearrange("p (t w) -> p t w", w=pitch)[:, :, 0:P]
+
+        for t in range(ROWS):
+            to_f32(t)
+        for first, rows, bias in ((8, SCALAR_ROWS, 1.0), (0, VECTOR_ROWS, 0.0)):
+            nc.scalar.activation(
+                out=dd[:, rows], in_=sums[:, first : first + 2], func=ACT.Abs_reciprocal_sqrt, bias=bias, scale=1.0
+            )
+        squares = m_flat[:].rearrange("p (a w) -> p a w", w=pitch)[:, :, 0:P]
         nc.vector.tensor_tensor(
-            out=squares,
-            in0=squares,
-            in1=identity[:].unsqueeze(1).to_broadcast([P, ROWS, P]),
-            op=ALU.add,
+            out=squares, in0=squares, in1=identity.unsqueeze(1).to_broadcast([P, 2, P]), op=ALU.add
         )
-        dd = keep.tile([P, ROWS], F32)
-        nc.vector.reciprocal(out=dd[:], in_=root[:])
         dd_cols = psum_x2.tile([P, NODES], F32, tag="x2")
-        for u in range(ROWS):
+        for u in (0, 2, 1, 3):
             nc.tensor.transpose(
                 out=dd_cols[:, u * P : (u + 1) * P],
-                in_=dd[:, dd_at[u] : dd_at[u] + 1].to_broadcast([P, P]),
-                identity=identity[:],
+                in_=dd[:, u : u + 1].to_broadcast([P, P]),
+                identity=identity,
             )
-        for n in range(SCALAR_REGROUPS):
-            regroup_x0(n)
         scaled = keep.tile([P, ROWS, NODES], F32)
-        for t in range(ROWS):
-            nc.vector.tensor_scalar(
-                out=scaled[:, t, :],
-                in0=m[:, t, :],
-                scalar1=dd[:, dd_at[t] : dd_at[t] + 1],
-                scalar2=None,
-                op0=ALU.mult,
-            )
+        nc.scalar.activation(out=scaled[:, 3, :], in_=m[:, 3, :], func=ACT.Copy, scale=dd[:, 3:4])
+        def scale_full(rows):
+            for t in rows:
+                nc.vector.tensor_scalar(
+                    out=scaled[:, t, :], in0=m[:, t, :], scalar1=dd[:, t : t + 1], scalar2=None, op0=ALU.mult
+                )
+
+        for n in (0, 1,):
+            regroup_x0("scalar", n)
+        regroup_x0("gpsimd", 2)
         s_grouped = keep.tile([P, NODES, ROWS], BF16, align_bytes=64)
         s_codes = keep.tile([P, NODES], U32, align_bytes=64)
         s_scales = keep.tile([P, NODES], U8, align_bytes=64)
@@ -166,17 +184,17 @@ def tile_dgcn_pa_kernel(tc, inputs, adj, out_0, out_1):
                 in_=s_grouped[:, cols, :].rearrange("p q t -> p (q t)"),
             )
 
+        scale_full((0, 2, 1))
         scale_s(0)
         scale_s(1)
         quantise_s(0)
-        scale_s(2)
-        quantise_s(1)
         quantise_x0(0)
+        quantise_s(1)
+        scale_s(2)
         quantise_x0(1)
         quantise_x0(2)
         scale_s(3)
         quantise_s(2)
-        regroup_x0(3)
         quantise_s(3)
 
         def multiply(pool, kind, pair, operand):
@@ -205,91 +223,143 @@ def tile_dgcn_pa_kernel(tc, inputs, adj, out_0, out_1):
         x1_grouped = {}
         x1_packed = {}
 
-        def bank_x1(unit, j):
-            b, pair = divmod(unit, PAIRS)
-            bank = multiply(psum_x1, "x1", pair, x0_packed[b * BLOCKS_PER_BATCH + j])
-            nc.scalar.copy(out=block_slice(x1[b], slice(2 * pair, 2 * pair + 2), j), in_=bank[:])
+        bank_of = {}
 
-        def bank_x2(unit, j):
+        def multiply_x1(unit, j):
+            b, pair = divmod(unit, PAIRS)
+            bank_of["x1", unit, j] = multiply(psum_x1, "x1", pair, x0_packed[b * BLOCKS_PER_BATCH + j])
+
+        def empty_x1(unit, j):
+            b, pair = divmod(unit, PAIRS)
+            nc.scalar.copy(out=block_slice(x1[b], slice(2 * pair, 2 * pair + 2), j), in_=bank_of["x1", unit, j][:])
+
+        def multiply_x2(unit, j):
+            b, pair = divmod(unit, PAIRS)
+            bank_of["x2", unit, j] = multiply(psum_x2, "x2", pair, x1_packed[b * BLOCKS_PER_BATCH + j])
+
+        def empty_x2(unit, j):
             b, pair = divmod(unit, PAIRS)
             pair_rows = slice(2 * pair, 2 * pair + 2)
-            bank = multiply(psum_x2, "x2", pair, x1_packed[b * BLOCKS_PER_BATCH + j])
             nc.vector.scalar_tensor_tensor(
                 out=block_slice(x2[b], pair_rows, j),
-                in0=bank[:],
+                in0=bank_of["x2", unit, j][:],
                 scalar=2.0,
                 in1=block_slice(x0[b], pair_rows, j),
                 op0=ALU.mult,
                 op1=ALU.subtract,
             )
 
-        def store_unit(dram, tiles, unit):
+        def store_x1(unit):
             b, pair = divmod(unit, PAIRS)
-            store_pair(dram, tiles[b], b, slice(2 * pair, 2 * pair + 2))
+            store_pair(out_0, x1[b], b, slice(2 * pair, 2 * pair + 2))
 
-        def interleave_x1(b, j):
+        def store_x2(unit):
+            b, pair = divmod(unit, PAIRS)
+            store_pair(out_1, x2[b], b, slice(2 * pair, 2 * pair + 2))
+
+        def interleave_x1(engine, b, j):
             n = b * BLOCKS_PER_BATCH + j
-            rows_first = block_slice(x1[b], slice(0, ROWS), j)
-            if j == 2:
-                x1_grouped[n] = swap_axes(b > 0, rows_first, "x1g", n)
-                return
-            tile = handoff.tile([P, BLOCK, ROWS], BF16, name="x1h_%d" % n, tag="x1h_%d" % j, align_bytes=64)
-            x1_grouped[n] = tile
-            if b == 0:
-                out, in_ = by_fours(rows_first, tile[:])
-                nc.vector.tensor_copy(out=out, in_=in_)
-            else:
-                nc.gpsimd.tensor_scalar(
-                    out=tile[:],
-                    in0=rows_first.rearrange("p t c -> p c t"),
-                    scalar1=1.0,
-                    scalar2=0.0,
-                    op0=ALU.mult,
-                    op1=ALU.add,
-                )
+            x1_grouped[n] = handoff.tile([P, BLOCK, ROWS], BF16, name="x1g_%d" % n, tag="x1g_%d" % j, align_bytes=64)
+            swap_axes(engine, block_slice(x1[b], slice(0, ROWS), j), x1_grouped[n])
 
         def quantise_x1(b, j):
             n = b * BLOCKS_PER_BATCH + j
             x1_packed[n] = quantise(x1_grouped[n], "x1", n)
 
-        for n in range(4, N_BLOCKS):
-            regroup_x0(n)
-            quantise_x0(n - 1)
-        quantise_x0(N_BLOCKS - 1)
+        BLOCKS = tuple(range(BLOCKS_PER_BATCH))
+        ORDER = (2, 1, 0)
+        x1_banks = [(unit, j) for unit in range(UNITS) for j in BLOCKS]
+        x2_banks = [(unit, j) for unit in range(UNITS) for j in ORDER]
 
-        ORDER = (1, 2, 0)
+        def regroup(engine, n):
+            return (("x0g", n), [("x0q", n - GROUPED)], regroup_x0, (engine, n))
 
-        def unit_x1(unit):
-            for j in range(BLOCKS_PER_BATCH):
-                bank_x1(unit, j)
-            store_unit(out_0, x1, unit)
+        def quant_x0(n):
+            return (("x0q", n), [("x0g", n)], quantise_x0, (n,))
 
-        EARLY = UNITS - PAIRS
-        for unit in range(EARLY):
-            unit_x1(unit)
-            if unit >= 4 and unit % PAIRS == 0:
-                interleave_x1(unit // PAIRS - 1, 2)
-        interleave_x1(0, 1)
-        interleave_x1(0, 2)
-        quantise_x1(0, 1)
-        interleave_x1(0, 0)
-        quantise_x1(0, 2)
-        quantise_x1(0, 0)
+        def interleave(engine, b, j):
+            rows = [("x1", b * PAIRS + pair, j) for pair in range(PAIRS)]
+            return (("x1g", b, j), rows + [("x1q", b - 1, j)], interleave_x1, (engine, b, j))
+
+        def quant_x1(b, j):
+            return (("x1q", b, j), [("x1g", b, j)], quantise_x1, (b, j))
+
+        def mult(kind, i):
+            banks = x1_banks if kind == "x1" else x2_banks
+            unit, j = banks[i]
+            b = unit // PAIRS
+            before = [("x0q", b * BLOCKS_PER_BATCH + j)] if kind == "x1" else [("x1q", b, j)]
+            if i >= BANKS:
+                before.append((kind,) + banks[i - BANKS])
+            return ((kind + "m", unit, j), before, multiply_x1 if kind == "x1" else multiply_x2, (unit, j))
+
+        def empty(kind, i):
+            unit, j = (x1_banks if kind == "x1" else x2_banks)[i]
+            return ((kind, unit, j), [(kind + "m", unit, j)], empty_x1 if kind == "x1" else empty_x2, (unit, j))
+
+        def store(kind, unit):
+            emptied = [(kind, unit, j) for j in BLOCKS]
+            return ((kind + "st", unit), emptied, store_x1 if kind == "x1" else store_x2, (unit,))
+
+        PER_BATCH = PAIRS * BLOCKS_PER_BATCH
+        early = EARLY_BATCHES * PER_BATCH
+        ON_VECTOR = EARLY_BLOCKS + 1
+
+        vector = [regroup("vector", BLOCKS_PER_BATCH)]
+        for n in range(BLOCKS_PER_BATCH + 1, ON_VECTOR):
+            vector += [regroup("vector", n), quant_x0(n - 1)]
+        vector.append(quant_x0(ON_VECTOR - 1))
+        first, second, third = ORDER
+        vector += [interleave("vector", 0, first), interleave("vector", 0, second), quant_x1(0, first)]
+        vector += [interleave("vector", 0, third), quant_x1(0, second), quant_x1(0, third)]
         for b in range(BATCH):
+            for i in range(b * PER_BATCH, (b + 1) * PER_BATCH):
+                if i % PER_BATCH == PER_BATCH - 1 and b + 1 < BATCH:
+                    vector.append(quant_x1(b + 1, first))
+                vector.append(empty("x2", i))
+                if b == 0 and i == 4:
+                    vector += [quant_x0(n) for n in range(ON_VECTOR, min(ON_VECTOR+0,N_BLOCKS))]
             if b + 1 < BATCH:
-                interleave_x1(b + 1, 0)
-                interleave_x1(b + 1, 1)
-            for pair in range(PAIRS):
-                for j in ORDER:
-                    bank_x2(b * PAIRS + pair, j)
-                    if b == 0:
-                        bank_x1(EARLY + pair, j)
-                store_unit(out_1, x2, b * PAIRS + pair)
-                if b == 0:
-                    store_unit(out_0, x1, EARLY + pair)
+                vector += [quant_x1(b + 1, second), quant_x1(b + 1, third)]
             if b == 0:
-                interleave_x1(2, 2)
-                interleave_x1(3, 2)
-            if b + 1 < BATCH:
-                for j in ORDER:
-                    quantise_x1(b + 1, j)
+                vector += [quant_x0(n) for n in range(ON_VECTOR+0, N_BLOCKS)]
+
+        scalar = [empty("x1", i) for i in range(early)]
+        scalar += [interleave("scalar", 1, first)]
+        scalar += [regroup("scalar", n) for n in range(ON_VECTOR, N_BLOCKS)]
+        scalar += [empty("x1", i) for i in range(early, early+3)]
+        scalar += [interleave("scalar", 2, first)]
+        scalar += [empty("x1", i) for i in range(early + 3, len(x1_banks))]
+        scalar += [interleave("scalar", 3, first)]
+
+        gpsimd = [interleave("gpsimd", b, j) for b in range(1, BATCH) for j in (third, second)]
+
+        tensor = [mult("x1", i) for i in range(early)]
+        L = [("x2",i) for i in range(2*PER_BATCH)]
+        X = [("x1",early+i) for i in range(PER_BATCH)]
+        at0=6
+        out = L[:at0]
+        rest = L[at0:]
+        while rest or X:
+            out += X[:1]; X = X[1:]
+            out += rest[:1]; rest = rest[1:]
+        tensor += [mult(k,i) for k,i in out]
+        tensor += [mult("x2", i) for i in range(2 * PER_BATCH, len(x2_banks))]
+
+        sync = [store("x1", unit) for unit in range(EARLY_BATCHES * PAIRS)]
+        sync += [store(k, u) for k, u in [("x2", 0), ("x2", 1), ("x1", 6), ("x2", 2), ("x1", 7)]]
+        sync += [store("x2", unit) for unit in range(3, UNITS)]
+
+        written = set([("x0q", n) for n in range(-GROUPED, BLOCKS_PER_BATCH)] + [("x1q", -1, j) for j in BLOCKS])
+        lists = [vector, scalar, gpsimd, tensor, sync]
+        at = [0] * len(lists)
+        while any(at[e] < len(lists[e]) for e in range(len(lists))):
+            moved = False
+            for e in range(len(lists)):
+                while at[e] < len(lists[e]) and all(x in written for x in lists[e][at[e]][1]):
+                    made, before, function, arguments = lists[e][at[e]]
+                    function(*arguments)
+                    written.add(made)
+                    at[e] += 1
+                    moved = True
+            assert moved

@@ -100,10 +100,13 @@ def tile_dgcn_pa_kernel(tc, inputs, adj, out_0, out_1):
         x0_grouped = {}
         x0_packed = {}
 
-        def regroup_x0(engine, n):
+        def regroup_x0(engine, n, after_vector=False):
             b, j = divmod(n, BLOCKS_PER_BATCH)
-            x0_grouped[n] = grouped.tile([P, BLOCK, ROWS], BF16, name="x0g_%d" % n, tag="x0g", align_bytes=64)
-            swap_axes(engine, block_slice(x0[b], slice(0, ROWS), j), x0_grouped[n])
+            tile = grouped.tile([P, BLOCK, ROWS], BF16, name="x0g_%d" % n, tag="x0g", align_bytes=64)
+            x0_grouped[n] = tile
+            if after_vector:
+                nc.vector.memset(tile[:, 0:1, :], 0.0)
+            swap_axes(engine, block_slice(x0[b], slice(0, ROWS), j), tile)
 
         def quantise_x0(n):
             x0_packed[n] = quantise(x0_grouped[n], "x0", n)
@@ -160,9 +163,8 @@ def tile_dgcn_pa_kernel(tc, inputs, adj, out_0, out_1):
                     out=scaled[:, t, :], in0=m[:, t, :], scalar1=dd[:, t : t + 1], scalar2=None, op0=ALU.mult
                 )
 
-        for n in (0, 1,):
+        for n in (0, 2,):
             regroup_x0("scalar", n)
-        regroup_x0("gpsimd", 2)
         s_grouped = keep.tile([P, NODES, ROWS], BF16, align_bytes=64)
         s_codes = keep.tile([P, NODES], U32, align_bytes=64)
         s_scales = keep.tile([P, NODES], U8, align_bytes=64)
@@ -184,15 +186,18 @@ def tile_dgcn_pa_kernel(tc, inputs, adj, out_0, out_1):
                 in_=s_grouped[:, cols, :].rearrange("p q t -> p (q t)"),
             )
 
-        scale_full((0, 2, 1))
+        scale_full((0, 2))
+        regroup_x0("gpsimd", 1, after_vector=True)
+        scale_full((1,))
         scale_s(0)
         scale_s(1)
         quantise_s(0)
         quantise_x0(0)
         quantise_s(1)
-        scale_s(2)
         quantise_x0(1)
+        regroup_x0("gpsimd", 3, after_vector=True)
         quantise_x0(2)
+        scale_s(2)
         scale_s(3)
         quantise_s(2)
         quantise_s(3)
@@ -305,8 +310,8 @@ def tile_dgcn_pa_kernel(tc, inputs, adj, out_0, out_1):
         early = EARLY_BATCHES * PER_BATCH
         ON_VECTOR = EARLY_BLOCKS + 1
 
-        vector = [regroup("vector", BLOCKS_PER_BATCH)]
-        for n in range(BLOCKS_PER_BATCH + 1, ON_VECTOR):
+        vector = [regroup("vector", 4), quant_x0(3)]
+        for n in range(5, ON_VECTOR):
             vector += [regroup("vector", n), quant_x0(n - 1)]
         vector.append(quant_x0(ON_VECTOR - 1))
         first, second, third = ORDER
@@ -316,13 +321,17 @@ def tile_dgcn_pa_kernel(tc, inputs, adj, out_0, out_1):
             for i in range(b * PER_BATCH, (b + 1) * PER_BATCH):
                 if i % PER_BATCH == PER_BATCH - 1 and b + 1 < BATCH:
                     vector.append(quant_x1(b + 1, first))
+                    if b == 0:
+                        vector += [quant_x0(n) for n in range(ON_VECTOR, ON_VECTOR + 1)]
                 vector.append(empty("x2", i))
                 if b == 0 and i == 4:
                     vector += [quant_x0(n) for n in range(ON_VECTOR, min(ON_VECTOR+0,N_BLOCKS))]
             if b + 1 < BATCH:
-                vector += [quant_x1(b + 1, second), quant_x1(b + 1, third)]
+                vector += [quant_x1(b + 1, second)]
             if b == 0:
-                vector += [quant_x0(n) for n in range(ON_VECTOR+0, N_BLOCKS)]
+                vector += [quant_x0(n) for n in range(ON_VECTOR + 1, N_BLOCKS)]
+            if b + 1 < BATCH:
+                vector += [quant_x1(b + 1, third)]
 
         scalar = [empty("x1", i) for i in range(early)]
         scalar += [interleave("scalar", 1, first)]
@@ -350,7 +359,7 @@ def tile_dgcn_pa_kernel(tc, inputs, adj, out_0, out_1):
         sync += [store(k, u) for k, u in [("x2", 0), ("x2", 1), ("x1", 6), ("x2", 2), ("x1", 7)]]
         sync += [store("x2", unit) for unit in range(3, UNITS)]
 
-        written = set([("x0q", n) for n in range(-GROUPED, BLOCKS_PER_BATCH)] + [("x1q", -1, j) for j in BLOCKS])
+        written = set([("x0g", n) for n in x0_grouped] + [("x0q", n) for n in range(-GROUPED, BLOCKS_PER_BATCH)] + [("x1q", -1, j) for j in BLOCKS])
         lists = [vector, scalar, gpsimd, tensor, sync]
         at = [0] * len(lists)
         while any(at[e] < len(lists[e]) for e in range(len(lists))):

@@ -52,8 +52,8 @@ def tile_dgcn_pa_kernel(tc, inputs, adj, out_0, out_1):
 
         adj_rows = keep.tile([P, ROWS, NODES], BF16, align_bytes=256)
         adj_view = adj.rearrange("(p t) i -> p t i", t=ROWS)
-        for t in range(ROWS):
-            nc.sync.dma_start(out=adj_rows[:, t, :], in_=adj_view[:, t, :])
+        for rows in (slice(0, 2), slice(2, ROWS)):
+            nc.sync.dma_start(out=adj_rows[:, rows, :], in_=adj_view[:, rows, :])
         x0 = []
         for b in range(BATCH):
             x0_b = keep.tile([P, ROWS, FEAT], BF16, name="x0_%d" % b, align_bytes=256)
@@ -72,10 +72,10 @@ def tile_dgcn_pa_kernel(tc, inputs, adj, out_0, out_1):
         def block_slice(tile, rows, j):
             return tile[:, rows, j * BLOCK : (j + 1) * BLOCK]
 
-        def swap_axes(engine, rows_first, tile):
+        def swap_axes(engine, rows_first, cols_first):
             if engine == "gpsimd":
                 nc.gpsimd.tensor_scalar(
-                    out=tile[:],
+                    out=cols_first,
                     in0=rows_first.rearrange("p t c -> p c t"),
                     scalar1=1.0,
                     scalar2=0.0,
@@ -83,7 +83,7 @@ def tile_dgcn_pa_kernel(tc, inputs, adj, out_0, out_1):
                     op1=ALU.add,
                 )
                 return
-            out, in_ = by_fours(rows_first, tile[:])
+            out, in_ = by_fours(rows_first, cols_first)
             if engine == "scalar":
                 nc.scalar.copy(out=out, in_=in_)
             else:
@@ -106,7 +106,12 @@ def tile_dgcn_pa_kernel(tc, inputs, adj, out_0, out_1):
             x0_grouped[n] = tile
             if after_vector:
                 nc.vector.memset(tile[:, 0:1, :], 0.0)
-            swap_axes(engine, block_slice(x0[b], slice(0, ROWS), j), tile)
+            if engine:
+                swap_axes(engine, block_slice(x0[b], slice(0, ROWS), j), tile[:])
+
+        def regroup_part(engine, n, cols):
+            b, j = divmod(n, BLOCKS_PER_BATCH)
+            swap_axes(engine, block_slice(x0[b], slice(0, ROWS), j)[:, :, cols], x0_grouped[n][:, cols, :])
 
         def quantise_x0(n):
             x0_packed[n] = quantise(x0_grouped[n], "x0", n)
@@ -165,6 +170,8 @@ def tile_dgcn_pa_kernel(tc, inputs, adj, out_0, out_1):
 
         for n in (0, 2,):
             regroup_x0("scalar", n)
+        regroup_x0(None, 4)
+        regroup_part("scalar", 4, slice(0, BLOCK // 2))
         s_grouped = keep.tile([P, NODES, ROWS], BF16, align_bytes=64)
         s_codes = keep.tile([P, NODES], U32, align_bytes=64)
         s_scales = keep.tile([P, NODES], U8, align_bytes=64)
@@ -265,7 +272,7 @@ def tile_dgcn_pa_kernel(tc, inputs, adj, out_0, out_1):
         def interleave_x1(engine, b, j):
             n = b * BLOCKS_PER_BATCH + j
             x1_grouped[n] = handoff.tile([P, BLOCK, ROWS], BF16, name="x1g_%d" % n, tag="x1g_%d" % j, align_bytes=64)
-            swap_axes(engine, block_slice(x1[b], slice(0, ROWS), j), x1_grouped[n])
+            swap_axes(engine, block_slice(x1[b], slice(0, ROWS), j), x1_grouped[n][:])
 
         def quantise_x1(b, j):
             n = b * BLOCKS_PER_BATCH + j
@@ -310,8 +317,8 @@ def tile_dgcn_pa_kernel(tc, inputs, adj, out_0, out_1):
         early = EARLY_BATCHES * PER_BATCH
         ON_VECTOR = EARLY_BLOCKS + 1
 
-        vector = [regroup("vector", 4), quant_x0(3)]
-        for n in range(5, ON_VECTOR):
+        vector = [(("x0g", 4), [], regroup_part, ("vector", 4, slice(BLOCK // 2, BLOCK))), regroup("vector", 5), quant_x0(3), quant_x0(4), quant_x0(5), regroup("vector", 6)]
+        for n in range(7, ON_VECTOR):
             vector += [regroup("vector", n), quant_x0(n - 1)]
         vector.append(quant_x0(ON_VECTOR - 1))
         first, second, third = ORDER
@@ -359,7 +366,7 @@ def tile_dgcn_pa_kernel(tc, inputs, adj, out_0, out_1):
         sync += [store(k, u) for k, u in [("x2", 0), ("x2", 1), ("x1", 6), ("x2", 2), ("x1", 7)]]
         sync += [store("x2", unit) for unit in range(3, UNITS)]
 
-        written = set([("x0g", n) for n in x0_grouped] + [("x0q", n) for n in range(-GROUPED, BLOCKS_PER_BATCH)] + [("x1q", -1, j) for j in BLOCKS])
+        written = set([("x0g", n) for n in x0_grouped if n != 4] + [("x0q", n) for n in range(-GROUPED, BLOCKS_PER_BATCH)] + [("x1q", -1, j) for j in BLOCKS])
         lists = [vector, scalar, gpsimd, tensor, sync]
         at = [0] * len(lists)
         while any(at[e] < len(lists[e]) for e in range(len(lists))):

@@ -60,10 +60,11 @@ def tile_dgcn_pa_kernel(tc, inputs, adj, out_0, out_1):
             nc.sync.dma_start(out=x0_b[:], in_=inputs[b].rearrange("(p t) f -> p t f", t=ROWS))
             x0.append(x0_b)
 
-        unit = keep.tile([P, (2 * ROWS - 2) * P], F32)
-        nc.gpsimd.memset(unit[:], 0.0)
+        unit = keep.tile([P, (2 * ROWS - 2) * P], F32, align_bytes=64)
         identity = unit[:, (ROWS - 1) * P : ROWS * P]
         make_identity(nc, identity)
+        nc.vector.memset(unit[:, 0 : (ROWS - 1) * P], 0.0)
+        nc.vector.memset(unit[:, ROWS * P :], 0.0)
         ones = keep.tile([P, 8], F32)
         nc.vector.memset(ones[:], 1.0)
         dummy = keep.tile([P, 8], F32)
@@ -100,18 +101,17 @@ def tile_dgcn_pa_kernel(tc, inputs, adj, out_0, out_1):
         x0_grouped = {}
         x0_packed = {}
 
-        def regroup_x0(engine, n, after_vector=False):
+        def regroup_x0(engine, n, cols=slice(0, BLOCK)):
             b, j = divmod(n, BLOCKS_PER_BATCH)
+            if n not in x0_grouped:
+                tile = grouped.tile([P, BLOCK, ROWS], BF16, name="x0g_%d" % n, tag="x0g", align_bytes=64)
+                x0_grouped[n] = tile
+            swap_axes(engine, block_slice(x0[b], slice(0, ROWS), j)[:, :, cols], x0_grouped[n][:, cols, :])
+
+        def release_gpsimd(n):
             tile = grouped.tile([P, BLOCK, ROWS], BF16, name="x0g_%d" % n, tag="x0g", align_bytes=64)
             x0_grouped[n] = tile
-            if after_vector:
-                nc.vector.memset(tile[:, 0:1, :], 0.0)
-            if engine:
-                swap_axes(engine, block_slice(x0[b], slice(0, ROWS), j), tile[:])
-
-        def regroup_part(engine, n, cols):
-            b, j = divmod(n, BLOCKS_PER_BATCH)
-            swap_axes(engine, block_slice(x0[b], slice(0, ROWS), j)[:, :, cols], x0_grouped[n][:, cols, :])
+            nc.vector.memset(tile[:, 0:1, :], 0.0)
 
         def quantise_x0(n):
             x0_packed[n] = quantise(x0_grouped[n], "x0", n)
@@ -168,10 +168,7 @@ def tile_dgcn_pa_kernel(tc, inputs, adj, out_0, out_1):
                     out=scaled[:, t, :], in0=m[:, t, :], scalar1=dd[:, t : t + 1], scalar2=None, op0=ALU.mult
                 )
 
-        for n in (0, 2,):
-            regroup_x0("scalar", n)
-        regroup_x0(None, 4)
-        regroup_part("scalar", 4, slice(0, BLOCK // 2))
+        regroup_x0("scalar", 0, slice(0, 256))
         s_grouped = keep.tile([P, NODES, ROWS], BF16, align_bytes=64)
         s_codes = keep.tile([P, NODES], U32, align_bytes=64)
         s_scales = keep.tile([P, NODES], U8, align_bytes=64)
@@ -194,7 +191,11 @@ def tile_dgcn_pa_kernel(tc, inputs, adj, out_0, out_1):
             )
 
         scale_full((0, 2))
-        regroup_x0("gpsimd", 1, after_vector=True)
+        release_gpsimd(1)
+        regroup_x0("gpsimd", 1, slice(0, 192))
+        regroup_x0("scalar", 1, slice(192, 256))
+        regroup_x0("scalar", 2, slice(0, 256))
+        regroup_x0("scalar", 4, slice(0, 128))
         scale_full((1,))
         scale_s(0)
         scale_s(1)
@@ -202,9 +203,8 @@ def tile_dgcn_pa_kernel(tc, inputs, adj, out_0, out_1):
         quantise_x0(0)
         quantise_s(1)
         quantise_x0(1)
-        regroup_x0("gpsimd", 3, after_vector=True)
-        quantise_x0(2)
         scale_s(2)
+        quantise_x0(2)
         scale_s(3)
         quantise_s(2)
         quantise_s(3)
@@ -317,7 +317,10 @@ def tile_dgcn_pa_kernel(tc, inputs, adj, out_0, out_1):
         early = EARLY_BATCHES * PER_BATCH
         ON_VECTOR = EARLY_BLOCKS + 1
 
-        vector = [(("x0g", 4), [], regroup_part, ("vector", 4, slice(BLOCK // 2, BLOCK))), regroup("vector", 5), quant_x0(3), quant_x0(4), quant_x0(5), regroup("vector", 6)]
+        def part(n, c0, c1):
+            return (("x0g", n), [("x0q", n - GROUPED)], regroup_x0, ("vector", n, slice(c0, c1)))
+
+        vector = [regroup("vector", 3), part(4, 128, 256), regroup("vector", 5), quant_x0(3), quant_x0(4), quant_x0(5), regroup("vector", 6)]
         for n in range(7, ON_VECTOR):
             vector += [regroup("vector", n), quant_x0(n - 1)]
         vector.append(quant_x0(ON_VECTOR - 1))
@@ -327,14 +330,14 @@ def tile_dgcn_pa_kernel(tc, inputs, adj, out_0, out_1):
         for b in range(BATCH):
             for i in range(b * PER_BATCH, (b + 1) * PER_BATCH):
                 if i % PER_BATCH == PER_BATCH - 1 and b + 1 < BATCH:
-                    vector.append(quant_x1(b + 1, first))
+                    if b in (0, 2): vector.append(quant_x1(b + 1, first))
                     if b == 0:
                         vector += [quant_x0(n) for n in range(ON_VECTOR, ON_VECTOR + 1)]
                 vector.append(empty("x2", i))
                 if b == 0 and i == 4:
                     vector += [quant_x0(n) for n in range(ON_VECTOR, min(ON_VECTOR+0,N_BLOCKS))]
             if b + 1 < BATCH:
-                vector += [quant_x1(b + 1, second)]
+                vector += [quant_x1(b + 1, j) for j in ((second,) if b in (0, 2) else (first, second))]
             if b == 0:
                 vector += [quant_x0(n) for n in range(ON_VECTOR + 1, N_BLOCKS)]
             if b + 1 < BATCH:
@@ -346,9 +349,9 @@ def tile_dgcn_pa_kernel(tc, inputs, adj, out_0, out_1):
         scalar += [empty("x1", i) for i in range(early, early+3)]
         scalar += [interleave("scalar", 2, first)]
         scalar += [empty("x1", i) for i in range(early + 3, len(x1_banks))]
-        scalar += [interleave("scalar", 3, first)]
+        scalar += [interleave("scalar", 3, first), interleave("scalar", 3, second)]
 
-        gpsimd = [interleave("gpsimd", b, j) for b in range(1, BATCH) for j in (third, second)]
+        gpsimd = [interleave("gpsimd", b, j) for b in range(1, BATCH) for j in (third, second) if (b, j) != (3, second)]
 
         tensor = [mult("x1", i) for i in range(early)]
         L = [("x2",i) for i in range(2*PER_BATCH)]
@@ -366,7 +369,7 @@ def tile_dgcn_pa_kernel(tc, inputs, adj, out_0, out_1):
         sync += [store(k, u) for k, u in [("x2", 0), ("x2", 1), ("x1", 6), ("x2", 2), ("x1", 7)]]
         sync += [store("x2", unit) for unit in range(3, UNITS)]
 
-        written = set([("x0g", n) for n in x0_grouped if n != 4] + [("x0q", n) for n in range(-GROUPED, BLOCKS_PER_BATCH)] + [("x1q", -1, j) for j in BLOCKS])
+        written = set([("x0g", n) for n in x0_grouped if n not in (4,)] + [("x0q", n) for n in range(-GROUPED, BLOCKS_PER_BATCH)] + [("x1q", -1, j) for j in BLOCKS])
         lists = [vector, scalar, gpsimd, tensor, sync]
         at = [0] * len(lists)
         while any(at[e] < len(lists[e]) for e in range(len(lists))):

@@ -116,9 +116,7 @@ def tile_dgcn_pa_kernel(tc, inputs, adj, out_0, out_1):
         def quantise_x0(n):
             x0_packed[n] = quantise(x0_grouped[n], "x0", n)
 
-        pitch = 2 * NODES + 2 * P
-        m_flat = keep.tile([P, 2 * pitch], F32)
-        m = m_flat[:, 0 : ROWS * NODES].rearrange("p (t c) -> p t c", t=ROWS)
+        m = keep.tile([P, ROWS, NODES], F32)
         sums = keep.tile([P, 16], F32)
         SCALAR_ROWS = slice(0, ROWS, 2)
         VECTOR_ROWS = slice(1, ROWS, 2)
@@ -149,10 +147,10 @@ def tile_dgcn_pa_kernel(tc, inputs, adj, out_0, out_1):
             nc.scalar.activation(
                 out=dd[:, rows], in_=sums[:, first : first + 2], func=ACT.Abs_reciprocal_sqrt, bias=bias, scale=1.0
             )
-        squares = m_flat[:].rearrange("p (a w) -> p a w", w=pitch)[:, :, 0:P]
-        nc.vector.tensor_tensor(
-            out=squares, in0=squares, in1=identity.unsqueeze(1).to_broadcast([P, 2, P]), op=ALU.add
-        )
+        for t in (0, 2):
+            square = m[:, t, t * P : (t + 1) * P]
+            nc.vector.tensor_tensor(out=square, in0=square, in1=identity, op=ALU.add)
+        warm = psum_x1.tile([P, NODES], F32, tag="x1")
         dd_cols = psum_x2.tile([P, NODES], F32, tag="x2")
         for u in (0, 2, 1, 3):
             nc.tensor.transpose(
@@ -160,8 +158,12 @@ def tile_dgcn_pa_kernel(tc, inputs, adj, out_0, out_1):
                 in_=dd[:, u : u + 1].to_broadcast([P, P]),
                 identity=identity,
             )
+        for i in range(3):
+            nc.tensor.matmul(out=warm[:], lhsT=adj_rows[:, 0, 0:P], rhs=adj_rows[:, 0, :], start=True, stop=True)
         scaled = keep.tile([P, ROWS, NODES], F32)
         nc.scalar.activation(out=scaled[:, 3, :], in_=m[:, 3, :], func=ACT.Copy, scale=dd[:, 3:4])
+        late = slice(NODES // 2, NODES)
+        nc.scalar.activation(out=scaled[:, 1, late], in_=m[:, 1, late], func=ACT.Copy, scale=dd[:, 1:2])
         def scale_full(rows):
             for t in rows:
                 nc.vector.tensor_scalar(
@@ -169,6 +171,8 @@ def tile_dgcn_pa_kernel(tc, inputs, adj, out_0, out_1):
                 )
 
         regroup_x0("scalar", 0, slice(0, 256))
+        regroup_x0("scalar", 2, slice(0, 256))
+        regroup_x0("scalar", 4, slice(0, 128))
         s_grouped = keep.tile([P, NODES, ROWS], BF16, align_bytes=64)
         s_codes = keep.tile([P, NODES], U32, align_bytes=64)
         s_scales = keep.tile([P, NODES], U8, align_bytes=64)
@@ -192,11 +196,11 @@ def tile_dgcn_pa_kernel(tc, inputs, adj, out_0, out_1):
 
         scale_full((0, 2))
         release_gpsimd(1)
-        regroup_x0("gpsimd", 1, slice(0, 192))
-        regroup_x0("scalar", 1, slice(192, 256))
-        regroup_x0("scalar", 2, slice(0, 256))
-        regroup_x0("scalar", 4, slice(0, 128))
-        scale_full((1,))
+        regroup_x0("gpsimd", 1, slice(0, 256))
+        soon = slice(0, NODES // 2)
+        nc.vector.tensor_scalar(
+            out=scaled[:, 1, soon], in0=m[:, 1, soon], scalar1=dd[:, 1:2], scalar2=None, op0=ALU.mult
+        )
         scale_s(0)
         scale_s(1)
         quantise_s(0)
@@ -320,7 +324,7 @@ def tile_dgcn_pa_kernel(tc, inputs, adj, out_0, out_1):
         def part(n, c0, c1):
             return (("x0g", n), [("x0q", n - GROUPED)], regroup_x0, ("vector", n, slice(c0, c1)))
 
-        vector = [regroup("vector", 3), part(4, 128, 256), regroup("vector", 5), quant_x0(3), quant_x0(4), quant_x0(5), regroup("vector", 6)]
+        vector = [regroup("vector", 3), part(4, 128, 256), quant_x0(3), regroup("vector", 5), quant_x0(4), quant_x0(5), regroup("vector", 6)]
         for n in range(7, ON_VECTOR):
             vector += [regroup("vector", n), quant_x0(n - 1)]
         vector.append(quant_x0(ON_VECTOR - 1))

@@ -143,7 +143,7 @@ def tile_dgcn_pa_kernel(tc, inputs, adj, out_0, out_1):
 
         for t in range(ROWS):
             to_f32(t)
-        for first, rows, bias in ((8, SCALAR_ROWS, 1.0), (0, VECTOR_ROWS, 0.0)):
+        for first, rows, bias in ((0, VECTOR_ROWS, 0.0), (8, SCALAR_ROWS, 1.0)):
             nc.scalar.activation(
                 out=dd[:, rows], in_=sums[:, first : first + 2], func=ACT.Abs_reciprocal_sqrt, bias=bias, scale=1.0
             )
@@ -161,18 +161,15 @@ def tile_dgcn_pa_kernel(tc, inputs, adj, out_0, out_1):
         for i in range(3):
             nc.tensor.matmul(out=warm[:], lhsT=adj_rows[:, 0, 0:P], rhs=adj_rows[:, 0, :], start=True, stop=True)
         scaled = keep.tile([P, ROWS, NODES], F32)
-        nc.scalar.activation(out=scaled[:, 3, :], in_=m[:, 3, :], func=ACT.Copy, scale=dd[:, 3:4])
-        late = slice(NODES // 2, NODES)
-        nc.scalar.activation(out=scaled[:, 1, late], in_=m[:, 1, late], func=ACT.Copy, scale=dd[:, 1:2])
+        HALF = NODES // 2
+        for t, c0, c1 in ((3, 0, 512), (1, 256, 512),):
+            nc.scalar.activation(out=scaled[:, t, c0:c1], in_=m[:, t, c0:c1], func=ACT.Copy, scale=dd[:, t : t + 1])
         def scale_full(rows):
             for t in rows:
                 nc.vector.tensor_scalar(
                     out=scaled[:, t, :], in0=m[:, t, :], scalar1=dd[:, t : t + 1], scalar2=None, op0=ALU.mult
                 )
 
-        regroup_x0("scalar", 0, slice(0, 256))
-        regroup_x0("scalar", 2, slice(0, 256))
-        regroup_x0("scalar", 4, slice(0, 128))
         s_grouped = keep.tile([P, NODES, ROWS], BF16, align_bytes=64)
         s_codes = keep.tile([P, NODES], U32, align_bytes=64)
         s_scales = keep.tile([P, NODES], U8, align_bytes=64)
@@ -194,12 +191,25 @@ def tile_dgcn_pa_kernel(tc, inputs, adj, out_0, out_1):
                 in_=s_grouped[:, cols, :].rearrange("p q t -> p (q t)"),
             )
 
-        scale_full((0, 2))
+        regroup_x0("scalar", 0, slice(0, 256))
+        regroup_x0("scalar", 2, slice(0, 256))
+        regroup_x0("scalar", 4, slice(0, 128))
+        nc.vector.tensor_scalar(
+            out=scaled[:, 1, 0:256], in0=m[:, 1, 0:256], scalar1=dd[:, 1 : 1 + 1], scalar2=None, op0=ALU.mult
+        )
+        nc.vector.tensor_scalar(
+            out=scaled[:, 0, 0:256], in0=m[:, 0, 0:256], scalar1=dd[:, 0 : 0 + 1], scalar2=None, op0=ALU.mult
+        )
         release_gpsimd(1)
         regroup_x0("gpsimd", 1, slice(0, 256))
-        soon = slice(0, NODES // 2)
         nc.vector.tensor_scalar(
-            out=scaled[:, 1, soon], in0=m[:, 1, soon], scalar1=dd[:, 1:2], scalar2=None, op0=ALU.mult
+            out=scaled[:, 2, 0:256], in0=m[:, 2, 0:256], scalar1=dd[:, 2 : 2 + 1], scalar2=None, op0=ALU.mult
+        )
+        nc.vector.tensor_scalar(
+            out=scaled[:, 0, 256:512], in0=m[:, 0, 256:512], scalar1=dd[:, 0 : 0 + 1], scalar2=None, op0=ALU.mult
+        )
+        nc.vector.tensor_scalar(
+            out=scaled[:, 2, 256:512], in0=m[:, 2, 256:512], scalar1=dd[:, 2 : 2 + 1], scalar2=None, op0=ALU.mult
         )
         scale_s(0)
         scale_s(1)

@@ -143,7 +143,7 @@ def tile_dgcn_pa_kernel(tc, inputs, adj, out_0, out_1):
 
         for t in range(ROWS):
             to_f32(t)
-        for first, rows, bias in ((0, VECTOR_ROWS, 0.0), (8, SCALAR_ROWS, 1.0)):
+        for first, rows, bias in ((8, SCALAR_ROWS, 1.0), (0, VECTOR_ROWS, 0.0)):
             nc.scalar.activation(
                 out=dd[:, rows], in_=sums[:, first : first + 2], func=ACT.Abs_reciprocal_sqrt, bias=bias, scale=1.0
             )

from contextlib import ExitStack

import concourse.mybir as mybir
from concourse.masks import make_identity

FP8X4 = mybir.dt.float8_e4m3fn_x4
BF16 = mybir.dt.bfloat16
F32 = mybir.dt.float32
U32 = mybir.dt.uint32
U8 = mybir.dt.uint8
ALU = mybir.AluOpType
ACT = mybir.ActivationFunctionType

P = 128
ROWS = 4
BATCH = 4
NODES = P * ROWS
FEAT = 768
BLOCK = 256
BLOCKS_PER_BATCH = FEAT // BLOCK
N_BLOCKS = BATCH * BLOCKS_PER_BATCH
PAIRS = ROWS // 2
GROUPED = 6
BANKS = 4
UNITS = BATCH * PAIRS

SCALAR_REGROUPS = 3
EARLY_BATCHES = 3
EARLY_BLOCKS = EARLY_BATCHES * BLOCKS_PER_BATCH

FLOPS = 2 * 2 * BATCH * NODES * NODES * FEAT


def by_fours(rows_first, cols_first):
    return (
        cols_first.rearrange("p (c i) t -> p c t i", i=4),
        rows_first.rearrange("p t (c i) -> p c t i", i=4),
    )


def tile_dgcn_pa_kernel(tc, inputs, adj, out_0, out_1):
    nc = tc.nc
    with ExitStack() as ctx:
        keep = ctx.enter_context(tc.tile_pool(name="keep", bufs=1))
        grouped = ctx.enter_context(tc.tile_pool(name="grouped", bufs=GROUPED))
        packed = ctx.enter_context(tc.tile_pool(name="packed", bufs=N_BLOCKS))
        results = ctx.enter_context(tc.tile_pool(name="results", bufs=BATCH))
        handoff = ctx.enter_context(tc.tile_pool(name="handoff", bufs=1))
        psum_x1 = ctx.enter_context(tc.psum_pool(name="psum_x1", bufs=BANKS))
        psum_x2 = ctx.enter_context(tc.psum_pool(name="psum_x2", bufs=BANKS))
        ctx.enter_context(tc.manual_schedule())

        adj_rows = keep.tile([P, ROWS, NODES], BF16, align_bytes=256)
        adj_view = adj.rearrange("(p t) i -> p t i", t=ROWS)
        for rows in (slice(0, 2), slice(2, ROWS)):
            nc.sync.dma_start(out=adj_rows[:, rows, :], in_=adj_view[:, rows, :])
        x0 = []
        for b in range(BATCH):
            x0_b = keep.tile([P, ROWS, FEAT], BF16, name="x0_%d" % b, align_bytes=256)
            nc.sync.dma_start(out=x0_b[:], in_=inputs[b].rearrange("(p t) f -> p t f", t=ROWS))
            x0.append(x0_b)

        unit = keep.tile([P, (2 * ROWS - 2) * P], F32, align_bytes=64)
        identity = unit[:, (ROWS - 1) * P : ROWS * P]
        make_identity(nc, identity)
        nc.vector.memset(unit[:, 0 : (ROWS - 1) * P], 0.0)
        nc.vector.memset(unit[:, ROWS * P :], 0.0)
        ones = keep.tile([P, 8], F32)
        nc.vector.memset(ones[:], 1.0)
        dummy = keep.tile([P, 8], F32)
        nc.scalar.activation(out=dummy[:], in_=ones[:], func=ACT.Abs_reciprocal_sqrt)

        def block_slice(tile, rows, j):
            return tile[:, rows, j * BLOCK : (j + 1) * BLOCK]

        def swap_axes(engine, rows_first, cols_first):
            if engine == "gpsimd":
                nc.gpsimd.tensor_scalar(
                    out=cols_first,
                    in0=rows_first.rearrange("p t c -> p c t"),
                    scalar1=1.0,
                    scalar2=0.0,
                    op0=ALU.mult,
                    op1=ALU.add,
                )
                return
            out, in_ = by_fours(rows_first, cols_first)
            if engine == "scalar":
                nc.scalar.copy(out=out, in_=in_)
            else:
                nc.vector.tensor_copy(out=out, in_=in_)

        def quantise(tile, kind, n):
            codes = packed.tile([P, BLOCK], U32, name="%s_codes_%d" % (kind, n), tag=kind + "_codes", align_bytes=64)
            scales = packed.tile([P, BLOCK], U8, name="%s_scales_%d" % (kind, n), tag=kind + "_scales", align_bytes=64)
            nc.vector.quantize_mx(
                out=codes[:].bitcast(FP8X4), scales=scales[:], in_=tile[:].rearrange("p f t -> p (f t)")
            )
            return codes, scales

        x0_grouped = {}
        x0_packed = {}

        def regroup_x0(engine, n, cols=slice(0, BLOCK)):
            b, j = divmod(n, BLOCKS_PER_BATCH)
            if n not in x0_grouped:
                tile = grouped.tile([P, BLOCK, ROWS], BF16, name="x0g_%d" % n, tag="x0g", align_bytes=64)
                x0_grouped[n] = tile
            swap_axes(engine, block_slice(x0[b], slice(0, ROWS), j)[:, :, cols], x0_grouped[n][:, cols, :])

        def release_gpsimd(n):
            tile = grouped.tile([P, BLOCK, ROWS], BF16, name="x0g_%d" % n, tag="x0g", align_bytes=64)
            x0_grouped[n] = tile
            nc.vector.memset(tile[:, 0:1, :], 0.0)

        def quantise_x0(n):
            x0_packed[n] = quantise(x0_grouped[n], "x0", n)

        m = keep.tile([P, ROWS, NODES], F32)
        sums = keep.tile([P, 16], F32)
        SCALAR_ROWS = slice(0, ROWS, 2)
        VECTOR_ROWS = slice(1, ROWS, 2)
        sum_at = {1: 0, 3: 1, 0: 8, 2: 9}
        dd = keep.tile([P, ROWS], F32)

        def to_f32(t):
            total = sums[:, sum_at[t] : sum_at[t] + 1]
            as_f32 = m[:, t, :].rearrange("p (u q) -> p u q", u=ROWS)
            row = adj_rows[:, t, :].rearrange("p (q u) -> p u q", u=ROWS)
            if t % 2 == 0:
                nc.scalar.activation(out=as_f32, in_=row, func=ACT.Copy, accum_out=total)
            else:
                window = unit[:, (ROWS - 1 - t) * P : (ROWS - 1 - t) * P + NODES]
                nc.vector.scalar_tensor_tensor(
                    out=as_f32,
                    in0=row,
                    scalar=1.0,
                    in1=window.rearrange("p (u q) -> p u q", u=ROWS),
                    op0=ALU.mult,
                    op1=ALU.add,
                    accum_out=total,
                )

        for t in range(ROWS):
            to_f32(t)
        for first, rows, bias in ((8, SCALAR_ROWS, 1.0), (0, VECTOR_ROWS, 0.0)):
            nc.scalar.activation(
                out=dd[:, rows], in_=sums[:, first : first + 2], func=ACT.Abs_reciprocal_sqrt, bias=bias, scale=1.0
            )
        for t in (0, 2):
            square = m[:, t, t * P : (t + 1) * P]
            nc.vector.tensor_tensor(out=square, in0=square, in1=identity, op=ALU.add)
        warm = psum_x1.tile([P, NODES], F32, tag="x1")
        dd_cols = psum_x2.tile([P, NODES], F32, tag="x2")
        for u in (0, 2, 1, 3):
            nc.tensor.transpose(
                out=dd_cols[:, u * P : (u + 1) * P],
                in_=dd[:, u : u + 1].to_broadcast([P, P]),
                identity=identity,
            )
        for i in range(3):
            nc.tensor.matmul(out=warm[:], lhsT=adj_rows[:, 0, 0:P], rhs=adj_rows[:, 0, :], start=True, stop=True)
        scaled = keep.tile([P, ROWS, NODES], F32)
        HALF = NODES // 2
        for t, c0, c1 in ((3, 0, 512), (1, 256, 512),):
            nc.scalar.activation(out=scaled[:, t, c0:c1], in_=m[:, t, c0:c1], func=ACT.Copy, scale=dd[:, t : t + 1])
        def scale_full(rows):
            for t in rows:
                nc.vector.tensor_scalar(
                    out=scaled[:, t, :], in0=m[:, t, :], scalar1=dd[:, t : t + 1], scalar2=None, op0=ALU.mult
                )

        s_grouped = keep.tile([P, NODES, ROWS], BF16, align_bytes=64)
        s_codes = keep.tile([P, NODES], U32, align_bytes=64)
        s_scales = keep.tile([P, NODES], U8, align_bytes=64)

        def scale_s(u):
            cols = slice(u * P, (u + 1) * P)
            nc.vector.tensor_tensor(
                out=s_grouped[:, cols, :],
                in0=scaled[:, :, cols].rearrange("p t q -> p q t"),
                in1=dd_cols[:, cols].unsqueeze(2).to_broadcast([P, P, ROWS]),
                op=ALU.mult,
            )

        def quantise_s(u):
            cols = slice(u * P, (u + 1) * P)
            nc.vector.quantize_mx(
                out=s_codes[:, cols].bitcast(FP8X4),
                scales=s_scales[:, cols],
                in_=s_grouped[:, cols, :].rearrange("p q t -> p (q t)"),
            )

        regroup_x0("scalar", 0, slice(0, 256))
        regroup_x0("scalar", 2, slice(0, 256))
        regroup_x0("scalar", 4, slice(0, 128))
        nc.vector.tensor_scalar(
            out=scaled[:, 1, 0:256], in0=m[:, 1, 0:256], scalar1=dd[:, 1 : 1 + 1], scalar2=None, op0=ALU.mult
        )
        nc.vector.tensor_scalar(
            out=scaled[:, 0, 0:256], in0=m[:, 0, 0:256], scalar1=dd[:, 0 : 0 + 1], scalar2=None, op0=ALU.mult
        )
        release_gpsimd(1)
        regroup_x0("gpsimd", 1, slice(0, 256))
        nc.vector.tensor_scalar(
            out=scaled[:, 2, 0:256], in0=m[:, 2, 0:256], scalar1=dd[:, 2 : 2 + 1], scalar2=None, op0=ALU.mult
        )
        nc.vector.tensor_scalar(
            out=scaled[:, 0, 256:512], in0=m[:, 0, 256:512], scalar1=dd[:, 0 : 0 + 1], scalar2=None, op0=ALU.mult
        )
        nc.vector.tensor_scalar(
            out=scaled[:, 2, 256:512], in0=m[:, 2, 256:512], scalar1=dd[:, 2 : 2 + 1], scalar2=None, op0=ALU.mult
        )
        scale_s(0)
        scale_s(1)
        quantise_s(0)
        quantise_x0(0)
        quantise_s(1)
        quantise_x0(1)
        scale_s(2)
        quantise_x0(2)
        scale_s(3)
        quantise_s(2)
        quantise_s(3)

        def multiply(pool, kind, pair, operand):
            codes, scales = operand
            bank = pool.tile([P, 2, BLOCK], F32, name=kind, tag=kind)
            for w in range(2):
                cols = slice((2 * pair + w) * P, (2 * pair + w + 1) * P)
                nc.tensor.matmul_mx(
                    out=bank[:, w, :],
                    lhsT=s_codes[:, cols].bitcast(FP8X4),
                    lhsT_scale=s_scales[:, cols],
                    rhs=codes[:].bitcast(FP8X4),
                    rhs_scale=scales[:],
                    start=True,
                    stop=True,
                )
            return bank

        def store_pair(dram, tile, b, pair_rows):
            nc.sync.dma_start(
                out=dram[b].rearrange("(p t) f -> p t f", t=ROWS)[:, pair_rows, :], in_=tile[:, pair_rows, :]
            )

        x1 = [results.tile([P, ROWS, FEAT], F32, name="x1_%d" % b, tag="x1", align_bytes=256) for b in range(BATCH)]
        x2 = [results.tile([P, ROWS, FEAT], F32, name="x2_%d" % b, tag="x2", align_bytes=256) for b in range(BATCH)]
        x1_grouped = {}
        x1_packed = {}

        bank_of = {}

        def multiply_x1(unit, j):
            b, pair = divmod(unit, PAIRS)
            bank_of["x1", unit, j] = multiply(psum_x1, "x1", pair, x0_packed[b * BLOCKS_PER_BATCH + j])

        def empty_x1(unit, j):
            b, pair = divmod(unit, PAIRS)
            nc.scalar.copy(out=block_slice(x1[b], slice(2 * pair, 2 * pair + 2), j), in_=bank_of["x1", unit, j][:])

        def multiply_x2(unit, j):
            b, pair = divmod(unit, PAIRS)
            bank_of["x2", unit, j] = multiply(psum_x2, "x2", pair, x1_packed[b * BLOCKS_PER_BATCH + j])

        def empty_x2(unit, j):
            b, pair = divmod(unit, PAIRS)
            pair_rows = slice(2 * pair, 2 * pair + 2)
            nc.vector.scalar_tensor_tensor(
                out=block_slice(x2[b], pair_rows, j),
                in0=bank_of["x2", unit, j][:],
                scalar=2.0,
                in1=block_slice(x0[b], pair_rows, j),
                op0=ALU.mult,
                op1=ALU.subtract,
            )

        def store_x1(unit):
            b, pair = divmod(unit, PAIRS)
            store_pair(out_0, x1[b], b, slice(2 * pair, 2 * pair + 2))

        def store_x2(unit):
            b, pair = divmod(unit, PAIRS)
            store_pair(out_1, x2[b], b, slice(2 * pair, 2 * pair + 2))

        def interleave_x1(engine, b, j):
            n = b * BLOCKS_PER_BATCH + j
            x1_grouped[n] = handoff.tile([P, BLOCK, ROWS], BF16, name="x1g_%d" % n, tag="x1g_%d" % j, align_bytes=64)
            swap_axes(engine, block_slice(x1[b], slice(0, ROWS), j), x1_grouped[n][:])

        def quantise_x1(b, j):
            n = b * BLOCKS_PER_BATCH + j
            x1_packed[n] = quantise(x1_grouped[n], "x1", n)

        BLOCKS = tuple(range(BLOCKS_PER_BATCH))
        ORDER = (2, 1, 0)
        x1_banks = [(unit, j) for unit in range(UNITS) for j in BLOCKS]
        x2_banks = [(unit, j) for unit in range(UNITS) for j in ORDER]

        def regroup(engine, n):
            return (("x0g", n), [("x0q", n - GROUPED)], regroup_x0, (engine, n))

        def quant_x0(n):
            return (("x0q", n), [("x0g", n)], quantise_x0, (n,))

        def interleave(engine, b, j):
            rows = [("x1", b * PAIRS + pair, j) for pair in range(PAIRS)]
            return (("x1g", b, j), rows + [("x1q", b - 1, j)], interleave_x1, (engine, b, j))

        def quant_x1(b, j):
            return (("x1q", b, j), [("x1g", b, j)], quantise_x1, (b, j))

        def mult(kind, i):
            banks = x1_banks if kind == "x1" else x2_banks
            unit, j = banks[i]
            b = unit // PAIRS
            before = [("x0q", b * BLOCKS_PER_BATCH + j)] if kind == "x1" else [("x1q", b, j)]
            if i >= BANKS:
                before.append((kind,) + banks[i - BANKS])
            return ((kind + "m", unit, j), before, multiply_x1 if kind == "x1" else multiply_x2, (unit, j))

        def empty(kind, i):
            unit, j = (x1_banks if kind == "x1" else x2_banks)[i]
            return ((kind, unit, j), [(kind + "m", unit, j)], empty_x1 if kind == "x1" else empty_x2, (unit, j))

        def store(kind, unit):
            emptied = [(kind, unit, j) for j in BLOCKS]
            return ((kind + "st", unit), emptied, store_x1 if kind == "x1" else store_x2, (unit,))

        PER_BATCH = PAIRS * BLOCKS_PER_BATCH
        early = EARLY_BATCHES * PER_BATCH
        ON_VECTOR = EARLY_BLOCKS + 1

        def part(n, c0, c1):
            return (("x0g", n), [("x0q", n - GROUPED)], regroup_x0, ("vector", n, slice(c0, c1)))

        vector = [regroup("vector", 3), part(4, 128, 256), quant_x0(3), regroup("vector", 5), quant_x0(4), quant_x0(5), regroup("vector", 6)]
        for n in range(7, ON_VECTOR):
            vector += [regroup("vector", n), quant_x0(n - 1)]
        vector.append(quant_x0(ON_VECTOR - 1))
        first, second, third = ORDER
        vector += [interleave("vector", 0, first), interleave("vector", 0, second), quant_x1(0, first)]
        vector += [interleave("vector", 0, third), quant_x1(0, second), quant_x1(0, third)]
        for b in range(BATCH):
            for i in range(b * PER_BATCH, (b + 1) * PER_BATCH):
                if i % PER_BATCH == PER_BATCH - 1 and b + 1 < BATCH:
                    if b in (0, 2): vector.append(quant_x1(b + 1, first))
                    if b == 0:
                        vector += [quant_x0(n) for n in range(ON_VECTOR, ON_VECTOR + 1)]
                vector.append(empty("x2", i))
                if b == 0 and i == 4:
                    vector += [quant_x0(n) for n in range(ON_VECTOR, min(ON_VECTOR+0,N_BLOCKS))]
            if b + 1 < BATCH:
                vector += [quant_x1(b + 1, j) for j in ((second,) if b in (0, 2) else (first, second))]
            if b == 0:
                vector += [quant_x0(n) for n in range(ON_VECTOR + 1, N_BLOCKS)]
            if b + 1 < BATCH:
                vector += [quant_x1(b + 1, third)]

        scalar = [empty("x1", i) for i in range(early)]
        scalar += [interleave("scalar", 1, first)]
        scalar += [regroup("scalar", n) for n in range(ON_VECTOR, N_BLOCKS)]
        scalar += [empty("x1", i) for i in range(early, early+3)]
        scalar += [interleave("scalar", 2, first)]
        scalar += [empty("x1", i) for i in range(early + 3, len(x1_banks))]
        scalar += [interleave("scalar", 3, first), interleave("scalar", 3, second)]

        gpsimd = [interleave("gpsimd", b, j) for b in range(1, BATCH) for j in (third, second) if (b, j) != (3, second)]

        tensor = [mult("x1", i) for i in range(early)]
        L = [("x2",i) for i in range(2*PER_BATCH)]
        X = [("x1",early+i) for i in range(PER_BATCH)]
        at0=6
        out = L[:at0]
        rest = L[at0:]
        while rest or X:
            out += X[:1]; X = X[1:]
            out += rest[:1]; rest = rest[1:]
        tensor += [mult(k,i) for k,i in out]
        tensor += [mult("x2", i) for i in range(2 * PER_BATCH, len(x2_banks))]

        sync = [store("x1", unit) for unit in range(EARLY_BATCHES * PAIRS)]
        sync += [store(k, u) for k, u in [("x2", 0), ("x2", 1), ("x1", 6), ("x2", 2), ("x1", 7)]]
        sync += [store("x2", unit) for unit in range(3, UNITS)]

        written = set([("x0g", n) for n in x0_grouped if n not in (4,)] + [("x0q", n) for n in range(-GROUPED, BLOCKS_PER_BATCH)] + [("x1q", -1, j) for j in BLOCKS])
        lists = [vector, scalar, gpsimd, tensor, sync]
        at = [0] * len(lists)
        while any(at[e] < len(lists[e]) for e in range(len(lists))):
            moved = False
            for e in range(len(lists)):
                while at[e] < len(lists[e]) and all(x in written for x in lists[e][at[e]][1]):
                    made, before, function, arguments = lists[e][at[e]]
                    function(*arguments)
                    written.add(made)
                    at[e] += 1
                    moved = True
            assert moved
